import numpy as np
import ml_dtypes


def mxq(x, axis, fmt="e4m3"):
    dtype, down = {"e4m3": (ml_dtypes.float8_e4m3fn, 7), "e5m2": (ml_dtypes.float8_e5m2, 14)}[fmt]
    v = np.moveaxis(np.asarray(x, np.float32).astype(ml_dtypes.bfloat16).astype(np.float64), axis, -1)
    blocks = v.reshape(v.shape[:-1] + (-1, 32))
    amax = np.abs(blocks).max(-1, keepdims=True)
    byte = np.maximum(np.where(amax > 0, np.frexp(amax)[1] - 1 + 127, 0) - down, 1)
    scale = np.exp2(byte - 127.0)
    codes = (blocks / scale).astype(np.float32).astype(dtype).astype(np.float64)
    return np.moveaxis((codes * scale).reshape(v.shape), -1, axis)


WIDE = False


def mx_kscale(k):
    if not WIDE:
        return np.ones(k)
    levels = np.array([10, -10, 5, -5, 0])
    if k % 512:
        return np.exp2(np.random.permutation(np.resize(levels, k // 32))).repeat(32)
    a = np.empty((k // 512, 16))
    for p in range(k // 512):
        a[p, :8] = np.random.permutation(np.resize(levels, 8))
        for g in range(8):
            far = levels[np.abs(levels - a[p, g]) >= 10]
            a[p, g + 8] = far[np.random.randint(len(far))]
    return np.exp2(a.ravel()).repeat(32)


BF16 = ml_dtypes.bfloat16


def bf(x):
    return np.asarray(x, np.float32).astype(BF16)


def f64(x):
    return np.asarray(x).astype(np.float64)


B, HC, WC, C, F = 128, 8, 4, 512, 128


def draw0():
    s = mx_kscale(C)
    x_crop = np.stack([np.random.standard_normal((B, HC, WC, C)), np.random.standard_normal((B, HC, WC, C))], axis=1)
    return {"x_crop": bf(x_crop * s),
            "W_r": bf(np.random.standard_normal((HC, WC, C, F)) * 0.5 / np.sqrt(C) / s[:, None]),
            "W_i": bf(np.random.standard_normal((HC, WC, C, F)) * 0.5 / np.sqrt(C) / s[:, None]),
            "b_r": bf(np.random.standard_normal(F) * 0.3),
            "b_i": bf(np.random.standard_normal(F) * 0.3)}


def core(x_crop, W_r, W_i, b_r, b_i):
    sp = f64(x_crop)
    xr = mxq(sp[:, 0].transpose(1, 2, 0, 3), 3, "e4m3")
    xi = mxq(sp[:, 1].transpose(1, 2, 0, 3), 3, "e4m3")
    wr = mxq(f64(W_r), 2, "e4m3")
    wi = mxq(f64(W_i), 2, "e4m3")
    rr = xr @ wr
    ii = xi @ wi
    ri = xr @ wi
    ir = xi @ wr
    r = rr - ii + f64(b_r)
    i = ri + ir + f64(b_i)
    y = np.stack([r.transpose(2, 0, 1, 3), i.transpose(2, 0, 1, 3)], axis=1)
    return np.maximum(y, 0.0)


def e4m3fn_bytes(y):
    return np.clip(np.asarray(y, np.float64), -448.0, 448.0).astype(np.float32).astype(ml_dtypes.float8_e4m3fn).view(np.uint8)


def e4m3fn_values(b):
    return np.asarray(b, np.uint8).view(ml_dtypes.float8_e4m3fn).astype(np.float64)


def setup_inputs():
    d = draw0()
    x0 = np.asarray(d['x_crop']).astype(np.float64)
    s = (np.max(np.abs(x0), axis=(0, 1, 2, 3), keepdims=True) / 448.0).astype(np.float32)
    out = {}
    for k, v in d.items():
        if k == 'x_crop':
            out['x_crop_bytes'] = e4m3fn_bytes(x0 / s.astype(np.float64))
            out['x_crop_scale'] = s
        else:
            out[k] = v
    return out


def reference(x_crop_bytes, x_crop_scale, W_r, W_i, b_r, b_i):
    return core(e4m3fn_values(x_crop_bytes) * x_crop_scale.astype(np.float64), W_r, W_i, b_r, b_i)

@@ -1,0 +1,301 @@
+from contextlib import ExitStack
+
+import concourse.mybir as mybir
+from concourse.masks import make_identity
+
+F32 = mybir.dt.float32
+BF16 = mybir.dt.bfloat16
+U32 = mybir.dt.uint32
+U8 = mybir.dt.uint8
+FP8 = mybir.dt.float8_e4m3fn
+FP8X4 = mybir.dt.float8_e4m3fn_x4
+ALU = mybir.AluOpType
+ACT = mybir.ActivationFunctionType
+
+B, HC, WC, C, F = 128, 8, 4, 512, 128
+P = 128
+GW = WC * C
+G_UNITS = 7
+V_SUM = (5, 7)
+FLOPS = 4 * 2 * B * HC * WC * C * F
+
+
+def tile_dot_pa_kernel(tc, x_crop_bytes, x_crop_scale, W_r, W_i, b_r, b_i, out):
+    nc = tc.nc
+    with ExitStack() as ctx:
+        const = ctx.enter_context(tc.tile_pool(name="const", bufs=1))
+        xb_pool = ctx.enter_context(tc.tile_pool(name="xb_pool", bufs=HC))
+        wr_pool = ctx.enter_context(tc.tile_pool(name="wr_pool", bufs=HC))
+        xw_pool = ctx.enter_context(tc.tile_pool(name="xw_pool", bufs=3))
+        xg_pool = ctx.enter_context(tc.tile_pool(name="xg_pool", bufs=2))
+        wg_pool = ctx.enter_context(tc.tile_pool(name="wg_pool", bufs=1))
+        cd_pool = ctx.enter_context(tc.tile_pool(name="cd_pool", bufs=2))
+        ep_pool = ctx.enter_context(tc.tile_pool(name="ep_pool", bufs=2))
+        ot_pool = ctx.enter_context(tc.tile_pool(name="ot_pool", bufs=3))
+        tx_pool = ctx.enter_context(tc.psum_pool(name="tx_pool", bufs=4))
+        acc_pool = ctx.enter_context(tc.psum_pool(name="acc_pool", bufs=1))
+        ctx.enter_context(tc.manual_schedule())
+
+        xbytes, wraw, xwide, xgrp, wgrp, txs = {}, {}, {}, {}, {}, {}
+        xcod, xscl, wcod, wscl = {}, {}, {}, {}
+        acc, tt, r1s, i1s, tos, ots = {}, {}, {}, {}, {}, {}
+
+        sct = const.tile([P, 1, 2, 2], F32, name="sct", tag="sct")
+        nc.scalar.dma_start(
+            out=sct[:].rearrange("p o u e -> p (o u e)"),
+            in_=x_crop_scale.rearrange("a b c d (p t) -> p (a b c d t)", t=4),
+        )
+        brb = const.tile([P, 1], BF16, name="brb", tag="brb")
+        bib = const.tile([P, 1], BF16, name="bib", tag="bib")
+        nc.scalar.dma_start(out=brb[:], in_=b_r.rearrange("(f o) -> f o", o=1))
+        nc.scalar.dma_start(out=bib[:], in_=b_i.rearrange("(f o) -> f o", o=1))
+        ident = const.tile([P, P], F32, name="ident", tag="ident")
+        make_identity(nc, ident[:])
+        warm = const.tile([P, 1], F32, name="warm", tag="warm")
+        warm2 = const.tile([P, 1], F32, name="warm2", tag="warm2")
+        nc.gpsimd.memset(warm[:], 0.0)
+        nc.scalar.activation(out=warm2[:], in_=warm[:], func=ACT.Relu)
+        brc = const.tile([P, 1], F32, name="brc", tag="brc")
+        bic = const.tile([P, 1], F32, name="bic", tag="bic")
+
+        def load_x_half(g, h):
+            if h == 0:
+                xbytes[g] = xb_pool.tile([P, 2 * GW], U8, name="xbytes", tag="xbytes")
+            nc.sync.dma_start(
+                out=xbytes[g][:].rearrange("p (c h n) -> p c h n", c=2, h=2)[:, :, h, :],
+                in_=x_crop_bytes[:, :, g, 2 * h:2 * h + 2, :].rearrange("b c w k -> b c (w k)"),
+            )
+
+        def load_x(g):
+            xb = xb_pool.tile([P, 2 * GW], U8, name="xbytes", tag="xbytes")
+            nc.sync.dma_start(
+                out=xb[:].rearrange("p (c n) -> p c n", c=2),
+                in_=x_crop_bytes[:, :, g, :, :].rearrange("b c w k -> b c (w k)"),
+            )
+            xbytes[g] = xb
+
+        def load_w(g, m):
+            if m == 0:
+                wraw[g] = wr_pool.tile([P, 2, WC, 4 * F], BF16, name="wraw", tag="wraw")
+            src = (W_r, W_i)[m]
+            nc.sync.dma_start(out=wraw[g][:, m], in_=src[g].rearrange("w (p j) f -> p w (j f)", j=4))
+
+        def cast(g, lo, hi, on_vector=False):
+            if lo == 0:
+                xwide[g] = xw_pool.tile([P, 2 * GW], BF16, name="xw", tag="xw", align_bytes=64)
+            dst = xwide[g][:, lo:hi]
+            src = xbytes[g][:, lo:hi].bitcast(FP8)
+            if on_vector:
+                nc.vector.tensor_copy(out=dst, in_=src)
+            else:
+                nc.scalar.copy(out=dst, in_=src)
+
+        def txp(g):
+            words = xwide[g][:].bitcast(F32)
+            for w in range(WC):
+                tx = tx_pool.tile([P, 4 * P], F32, name="tx", tag="tx")
+                for u in range(2):
+                    for c in range(2):
+                        off = (c * WC + w) * (C // 2)
+                        nc.tensor.transpose(
+                            tx[:, (2 * u + c) * P:(2 * u + c + 1) * P],
+                            words[:, off + u:off + C // 2:2],
+                            ident[:],
+                        )
+                txs[g, w] = tx
+
+        def em(g):
+            xg = xg_pool.tile([P, 2 * GW], BF16, name="xg", tag="xg", align_bytes=64)
+            for w in range(WC):
+                nc.vector.tensor_tensor(
+                    out=xg[:, w * 2 * C:(w + 1) * 2 * C].rearrange("p (n u e) -> p n u e", u=2, e=2),
+                    in0=txs[g, w][:].bitcast(BF16).rearrange("p (u n e) -> p n u e", u=2, e=2),
+                    in1=sct[:].to_broadcast([P, 2 * P, 2, 2]),
+                    op=ALU.mult,
+                )
+            xgrp[g] = xg
+
+        def il_views(g, m, w0, w1):
+            dst = wgrp[g][:, (m * WC + w0) * C:(m * WC + w1) * C].rearrange("p (w f j) -> p w f j", w=w1 - w0, j=4)
+            src = wraw[g][:, m, w0:w1, :].rearrange("p w (j f) -> p w f j", j=4)
+            return dst, src
+
+        def wil_g(g):
+            wgrp[g] = wg_pool.tile([P, 2 * GW], BF16, name="wg", tag="wg", align_bytes=64)
+            if g == 0:
+                views = [il_views(g, 0, 0, WC), il_views(g, 1, 0, G_UNITS - WC)]
+            else:
+                views = [(
+                    wgrp[g][:, 0:G_UNITS * C].rearrange("p (w f j) -> p w f j", w=G_UNITS, j=4),
+                    wraw[g][:].rearrange("p m w n -> p (m w) n")[:, 0:G_UNITS, :].rearrange("p w (j f) -> p w f j", j=4),
+                )]
+            for dst, src in views:
+                nc.gpsimd.tensor_scalar(out=dst, in0=src, scalar1=1.0, scalar2=0.0, op0=ALU.mult, op1=ALU.add)
+
+        def wil_s(g):
+            dst, src = il_views(g, 1, G_UNITS - WC, WC)
+            nc.scalar.copy(out=dst, in_=src)
+
+        def quant_x(g):
+            cod = cd_pool.tile([P, 2 * WC * P], U32, name="xc", tag="xc", align_bytes=64)
+            scl = cd_pool.tile([P, 2 * WC * P], U8, name="xs", tag="xs", align_bytes=64)
+            nc.vector.quantize_mx(out=cod[:].bitcast(FP8X4), scales=scl[:], in_=xgrp[g][:])
+            xcod[g], xscl[g] = cod, scl
+
+        def quant_w(g):
+            cod = cd_pool.tile([P, 2 * WC * F], U32, name="wc", tag="wc", align_bytes=64)
+            scl = cd_pool.tile([P, 2 * WC * F], U8, name="ws", tag="ws", align_bytes=64)
+            nc.vector.quantize_mx(out=cod[:].bitcast(FP8X4), scales=scl[:], in_=wgrp[g][:])
+            wcod[g], wscl[g] = cod, scl
+
+        def mm(g):
+            rr = acc_pool.tile([P, WC * P], F32, name="rr", tag="rr")
+            ii = acc_pool.tile([P, WC * P], F32, name="ii", tag="ii")
+            pi = acc_pool.tile([P, WC * P], F32, name="pi", tag="pi")
+
+            def mx(dst, w, m, c, start, stop):
+                ws_ = slice((m * WC + w) * F, (m * WC + w + 1) * F)
+                xs_ = slice((2 * w + c) * P, (2 * w + c + 1) * P)
+                nc.tensor.matmul_mx(
+                    out=dst[:, w * P:(w + 1) * P],
+                    lhsT=wcod[g][:, ws_].bitcast(FP8X4),
+                    lhsT_scale=wscl[g][:, ws_],
+                    rhs=xcod[g][:, xs_].bitcast(FP8X4),
+                    rhs_scale=xscl[g][:, xs_],
+                    start=start,
+                    stop=stop,
+                )
+
+            for w in range(WC):
+                mx(ii, w, 1, 1, True, True)
+            for w in range(WC):
+                mx(rr, w, 0, 0, True, True)
+            for w in range(WC):
+                mx(pi, w, 0, 1, True, False)
+                mx(pi, w, 1, 0, False, True)
+            acc[g] = (rr, ii, pi)
+
+        def e1t(g):
+            t = ep_pool.tile([P, WC * P], F32, name="t", tag="t")
+            nc.scalar.activation(out=t[:], in_=acc[g][1][:], func=ACT.Identity, bias=brc[:], scale=-1.0)
+            tt[g] = t
+            if g not in V_SUM:
+                r = ep_pool.tile([P, WC * P], F32, name="r1", tag="r1")
+                nc.scalar.copy(out=r[:], in_=acc[g][0][:])
+                r1s[g] = r
+
+        def e1i(g):
+            i1 = ep_pool.tile([P, WC * P], F32, name="i1", tag="i1")
+            nc.scalar.activation(out=i1[:], in_=acc[g][2][:], func=ACT.Relu, bias=bic[:], scale=1.0)
+            i1s[g] = i1
+
+        def r1(g):
+            if g not in V_SUM:
+                return
+            r = ep_pool.tile([P, WC * P], F32, name="r1", tag="r1")
+            nc.vector.tensor_tensor(out=r[:], in0=acc[g][0][:], in1=tt[g][:], op=ALU.add)
+            r1s[g] = r
+
+        def tout(g, src, spare=False):
+            if spare:
+                to = tx_pool.tile([P, WC * F], F32, name="tx", tag="tx")
+            else:
+                to = acc_pool.tile([P, WC * F], F32, name="to", tag="to")
+            for w in range(WC):
+                if src is r1s and g not in V_SUM:
+                    nc.tensor.matmul(
+                        to[:, w * F:(w + 1) * F], lhsT=r1s[g][:, w * P:(w + 1) * P], rhs=ident[:],
+                        start=True, stop=False, is_transpose=True,
+                    )
+                    nc.tensor.matmul(
+                        to[:, w * F:(w + 1) * F], lhsT=tt[g][:, w * P:(w + 1) * P], rhs=ident[:],
+                        start=False, stop=True, is_transpose=True,
+                    )
+                else:
+                    nc.tensor.transpose(to[:, w * F:(w + 1) * F], src[g][:, w * P:(w + 1) * P], ident[:])
+            return to
+
+        def e2i(g):
+            ots[g] = ot_pool.tile([P, 2 * WC * F], F32, name="ot", tag="ot")
+            nc.scalar.copy(out=ots[g][:, WC * F:], in_=tos[g][:])
+
+        def e2r(g):
+            nc.scalar.activation(out=ots[g][:, 0:WC * F], in_=tos[g][:], func=ACT.Relu)
+            nc.sync.dma_start(
+                out=out[:, :, g, :, :].rearrange("b c w f -> b c (w f)"),
+                in_=ots[g][:].rearrange("p (c n) -> p c n", c=2),
+            )
+
+        load_x_half(0, 0)
+        load_w(0, 0)
+        load_x_half(0, 1)
+        load_w(0, 1)
+        load_x(1)
+        for g in range(2, HC):
+            load_x(g)
+            load_w(g - 1, 0)
+            load_w(g - 1, 1)
+        load_w(HC - 1, 0)
+        load_w(HC - 1, 1)
+
+        def has(g):
+            return 0 <= g < HC
+
+        cast(0, 0, GW // 2, on_vector=True)
+        cast(0, GW, GW + GW // 2, on_vector=True)
+        cast(0, GW // 2, GW)
+        cast(0, GW + GW // 2, 2 * GW)
+        txp(0)
+        wil_g(0)
+        cast(1, 0, GW // 2)
+        cast(1, GW, GW + GW // 2)
+        cast(1, GW // 2, GW)
+        cast(1, GW + GW // 2, 2 * GW)
+        wil_s(0)
+        nc.scalar.copy(out=brc[:], in_=brb[:])
+        nc.scalar.copy(out=bic[:], in_=bib[:])
+        em(0)
+        txp(1)
+        last = HC - 1
+        for j in range(last):
+            quant_x(j)
+            quant_w(j)
+            if has(j - 1):
+                r1(j - 1)
+            wil_g(j + 1)
+            if has(j + 2):
+                cast(j + 2, 0, GW)
+            wil_s(j + 1)
+            if has(j - 1):
+                e2i(j - 1)
+            mm(j)
+            if has(j - 1):
+                tos[j - 1] = tout(j - 1, r1s)
+            e1t(j)
+            if has(j + 2):
+                cast(j + 2, GW, 2 * GW)
+            e1i(j)
+            if has(j - 1):
+                e2r(j - 1)
+            em(j + 1)
+            if has(j + 2):
+                txp(j + 2)
+            tos[j] = tout(j, i1s)
+
+        quant_x(last)
+        quant_w(last)
+        r1(last - 1)
+        e2i(last - 1)
+        tos[last - 1] = tout(last - 1, r1s)
+        mm(last)
+        e1t(last)
+        e2r(last - 1)
+        e1i(last)
+        r1(last)
+        tr_last = tout(last, r1s, spare=True)
+        ti_last = tout(last, i1s, spare=True)
+        ot = ot_pool.tile([P, 2 * WC * F], F32, name="ot", tag="ot")
+        nc.scalar.activation(out=ot[:, 0:WC * F], in_=tr_last[:], func=ACT.Relu)
+        nc.sync.dma_start(out=out[:, 0, last, :, :].rearrange("b w f -> b (w f)"), in_=ot[:, 0:WC * F])
+        nc.vector.tensor_copy(out=ot[:, WC * F:], in_=ti_last[:])
+        nc.scalar.dma_start(out=out[:, 1, last, :, :].rearrange("b w f -> b (w f)"), in_=ot[:, WC * F:])

@@ -15,9 +15,19 @@ ACT = mybir.ActivationFunctionType
 B, HC, WC, C, F = 128, 8, 4, 512, 128
 P = 128
 GW = WC * C
-G_UNITS = 7
-V_SUM = (5, 7)
 FLOPS = 4 * 2 * B * HC * WC * C * F
+
+V_SUM = (5,)
+G_UNITS = (7, 7, 7, 7, 7, 7, 7, 5)
+PE_UNITS = (0, 0, 0, 0, 0, 0, 0, 0)
+HEAD = 0
+TAIL = 2
+SHAKE = 0
+QW_FIRST = 0
+XW_BUFS = 3
+IL4 = 0
+WS0_EARLY = 0
+PE0_AT = 0
 
 
 def tile_dot_pa_kernel(tc, x_crop_bytes, x_crop_scale, W_r, W_i, b_r, b_i, out):
@@ -26,8 +36,8 @@ def tile_dot_pa_kernel(tc, x_crop_bytes, x_crop_scale, W_r, W_i, b_r, b_i, out):
         const = ctx.enter_context(tc.tile_pool(name="const", bufs=1))
         xb_pool = ctx.enter_context(tc.tile_pool(name="xb_pool", bufs=HC))
         wr_pool = ctx.enter_context(tc.tile_pool(name="wr_pool", bufs=HC))
-        xw_pool = ctx.enter_context(tc.tile_pool(name="xw_pool", bufs=3))
-        xg_pool = ctx.enter_context(tc.tile_pool(name="xg_pool", bufs=2))
+        xw_pool = ctx.enter_context(tc.tile_pool(name="xw_pool", bufs=XW_BUFS))
+        xg_pool = ctx.enter_context(tc.tile_pool(name="xg_pool", bufs=3 if SHAKE else 2))
         wg_pool = ctx.enter_context(tc.tile_pool(name="wg_pool", bufs=1))
         cd_pool = ctx.enter_context(tc.tile_pool(name="cd_pool", bufs=2))
         ep_pool = ctx.enter_context(tc.tile_pool(name="ep_pool", bufs=2))
@@ -36,7 +46,7 @@ def tile_dot_pa_kernel(tc, x_crop_bytes, x_crop_scale, W_r, W_i, b_r, b_i, out):
         acc_pool = ctx.enter_context(tc.psum_pool(name="acc_pool", bufs=1))
         ctx.enter_context(tc.manual_schedule())
 
-        xbytes, wraw, xwide, xgrp, wgrp, txs = {}, {}, {}, {}, {}, {}
+        xbytes, wraw, xwide, xgrp, wgrp, txs, wps = {}, {}, {}, {}, {}, {}, {}
         xcod, xscl, wcod, wscl = {}, {}, {}, {}
         acc, tt, r1s, i1s, tos, ots = {}, {}, {}, {}, {}, {}
 
@@ -51,6 +61,9 @@ def tile_dot_pa_kernel(tc, x_crop_bytes, x_crop_scale, W_r, W_i, b_r, b_i, out):
         nc.scalar.dma_start(out=bib[:], in_=b_i.rearrange("(f o) -> f o", o=1))
         ident = const.tile([P, P], F32, name="ident", tag="ident")
         make_identity(nc, ident[:])
+        if sum(PE_UNITS):
+            identb = const.tile([P, P], BF16, name="identb", tag="identb")
+            nc.vector.tensor_copy(out=identb[:], in_=ident[:])
         warm = const.tile([P, 1], F32, name="warm", tag="warm")
         warm2 = const.tile([P, 1], F32, name="warm2", tag="warm2")
         nc.gpsimd.memset(warm[:], 0.0)
@@ -58,21 +71,13 @@ def tile_dot_pa_kernel(tc, x_crop_bytes, x_crop_scale, W_r, W_i, b_r, b_i, out):
         brc = const.tile([P, 1], F32, name="brc", tag="brc")
         bic = const.tile([P, 1], F32, name="bic", tag="bic")
 
-        def load_x_half(g, h):
-            if h == 0:
+        def load_x_px(g, w0, w1):
+            if w0 == 0:
                 xbytes[g] = xb_pool.tile([P, 2 * GW], U8, name="xbytes", tag="xbytes")
             nc.sync.dma_start(
-                out=xbytes[g][:].rearrange("p (c h n) -> p c h n", c=2, h=2)[:, :, h, :],
-                in_=x_crop_bytes[:, :, g, 2 * h:2 * h + 2, :].rearrange("b c w k -> b c (w k)"),
+                out=xbytes[g][:].rearrange("p (c n) -> p c n", c=2)[:, :, w0 * C:w1 * C],
+                in_=x_crop_bytes[:, :, g, w0:w1, :].rearrange("b c w k -> b c (w k)"),
             )
-
-        def load_x(g):
-            xb = xb_pool.tile([P, 2 * GW], U8, name="xbytes", tag="xbytes")
-            nc.sync.dma_start(
-                out=xb[:].rearrange("p (c n) -> p c n", c=2),
-                in_=x_crop_bytes[:, :, g, :, :].rearrange("b c w k -> b c (w k)"),
-            )
-            xbytes[g] = xb
 
         def load_w(g, m):
             if m == 0:
@@ -81,7 +86,7 @@ def tile_dot_pa_kernel(tc, x_crop_bytes, x_crop_scale, W_r, W_i, b_r, b_i, out):
             nc.sync.dma_start(out=wraw[g][:, m], in_=src[g].rearrange("w (p j) f -> p w (j f)", j=4))
 
         def cast(g, lo, hi, on_vector=False):
-            if lo == 0:
+            if g not in xwide:
                 xwide[g] = xw_pool.tile([P, 2 * GW], BF16, name="xw", tag="xw", align_bytes=64)
             dst = xwide[g][:, lo:hi]
             src = xbytes[g][:, lo:hi].bitcast(FP8)
@@ -90,9 +95,13 @@ def tile_dot_pa_kernel(tc, x_crop_bytes, x_crop_scale, W_r, W_i, b_r, b_i, out):
             else:
                 nc.scalar.copy(out=dst, in_=src)
 
-        def txp(g):
+        def cast_px(g, w0, w1, on_vector=False):
+            cast(g, w0 * C, w1 * C, on_vector)
+            cast(g, GW + w0 * C, GW + w1 * C, on_vector)
+
+        def txp(g, ws=(0, 1, 2, 3)):
             words = xwide[g][:].bitcast(F32)
-            for w in range(WC):
+            for w in ws:
                 tx = tx_pool.tile([P, 4 * P], F32, name="tx", tag="tx")
                 for u in range(2):
                     for c in range(2):
@@ -104,43 +113,74 @@ def tile_dot_pa_kernel(tc, x_crop_bytes, x_crop_scale, W_r, W_i, b_r, b_i, out):
                         )
                 txs[g, w] = tx
 
-        def em(g):
-            xg = xg_pool.tile([P, 2 * GW], BF16, name="xg", tag="xg", align_bytes=64)
-            for w in range(WC):
+        def new_xg(g):
+            xgrp[g] = xg_pool.tile([P, 2 * GW], BF16, name="xg", tag="xg", align_bytes=64)
+
+        def em(g, ws=(0, 1, 2, 3)):
+            if g not in xgrp:
+                new_xg(g)
+            xg = xgrp[g]
+            for w in ws:
                 nc.vector.tensor_tensor(
                     out=xg[:, w * 2 * C:(w + 1) * 2 * C].rearrange("p (n u e) -> p n u e", u=2, e=2),
                     in0=txs[g, w][:].bitcast(BF16).rearrange("p (u n e) -> p n u e", u=2, e=2),
                     in1=sct[:].to_broadcast([P, 2 * P, 2, 2]),
                     op=ALU.mult,
                 )
-            xgrp[g] = xg
 
-        def il_views(g, m, w0, w1):
-            dst = wgrp[g][:, (m * WC + w0) * C:(m * WC + w1) * C].rearrange("p (w f j) -> p w f j", w=w1 - w0, j=4)
-            src = wraw[g][:, m, w0:w1, :].rearrange("p w (j f) -> p w f j", j=4)
+        def il_views(g, u0, u1):
+            if IL4:
+                dst = wgrp[g][:, u0 * C:u1 * C].rearrange("p (w c i j) -> p w c j i", w=u1 - u0, j=4, i=4)
+                src = wraw[g][:].rearrange("p m w n -> p (m w) n")[:, u0:u1, :].rearrange("p w (j c i) -> p w c j i", j=4, i=4)
+                return dst, src
+            dst = wgrp[g][:, u0 * C:u1 * C].rearrange("p (w f j) -> p w f j", w=u1 - u0, j=4)
+            src = wraw[g][:].rearrange("p m w n -> p (m w) n")[:, u0:u1, :].rearrange("p w (j f) -> p w f j", j=4)
             return dst, src
 
-        def wil_g(g):
-            wgrp[g] = wg_pool.tile([P, 2 * GW], BF16, name="wg", tag="wg", align_bytes=64)
-            if g == 0:
-                views = [il_views(g, 0, 0, WC), il_views(g, 1, 0, G_UNITS - WC)]
+        def new_wg(g):
+            if SHAKE:
+                wgrp[g] = xg_pool.tile([P, 2 * GW], BF16, name="xg", tag="xg", align_bytes=64)
             else:
-                views = [(
-                    wgrp[g][:, 0:G_UNITS * C].rearrange("p (w f j) -> p w f j", w=G_UNITS, j=4),
-                    wraw[g][:].rearrange("p m w n -> p (m w) n")[:, 0:G_UNITS, :].rearrange("p w (j f) -> p w f j", j=4),
-                )]
-            for dst, src in views:
+                wgrp[g] = wg_pool.tile([P, 2 * GW], BF16, name="wg", tag="wg", align_bytes=64)
+
+        def wil_g(g, cuts=None):
+            if g not in wgrp:
+                new_wg(g)
+            cuts = cuts or (0, G_UNITS[g])
+            for a, b_ in zip(cuts[:-1], cuts[1:]):
+                dst, src = il_views(g, a, b_)
                 nc.gpsimd.tensor_scalar(out=dst, in0=src, scalar1=1.0, scalar2=0.0, op0=ALU.mult, op1=ALU.add)
 
         def wil_s(g):
-            dst, src = il_views(g, 1, G_UNITS - WC, WC)
-            nc.scalar.copy(out=dst, in_=src)
+            u0 = G_UNITS[g] + PE_UNITS[g]
+            if u0 < 8:
+                dst, src = il_views(g, u0, 8)
+                nc.scalar.copy(out=dst, in_=src)
 
-        def quant_x(g):
-            cod = cd_pool.tile([P, 2 * WC * P], U32, name="xc", tag="xc", align_bytes=64)
-            scl = cd_pool.tile([P, 2 * WC * P], U8, name="xs", tag="xs", align_bytes=64)
-            nc.vector.quantize_mx(out=cod[:].bitcast(FP8X4), scales=scl[:], in_=xgrp[g][:])
-            xcod[g], xscl[g] = cod, scl
+        def wpe_mm(g, tags=("ii", "rr")):
+            wps[g] = []
+            for k in range(0, PE_UNITS[g], 2):
+                n = min(2, PE_UNITS[g] - k)
+                wp = acc_pool.tile([P, n * C], BF16, name="wp", tag=tags[k // 2])
+                for i in range(n):
+                    u = G_UNITS[g] + k + i
+                    nc.tensor.matmul(
+                        wp[:, i * C:(i + 1) * C], lhsT=identb[:],
+                        rhs=wraw[g][:].rearrange("p m w n -> p (m w) n")[:, u, :].rearrange("p (j f) -> p f j", j=4),
+                        start=True, stop=True,
+                    )
+                wps[g].append((G_UNITS[g] + k, n, wp))
+
+        def wpe_cp(g):
+            for u, n, wp in wps.get(g, []):
+                nc.scalar.copy(out=wgrp[g][:, u * C:(u + n) * C], in_=wp[:])
+
+        def quant_x(g, h=None):
+            if g not in xcod:
+                xcod[g] = cd_pool.tile([P, 2 * WC * P], U32, name="xc", tag="xc", align_bytes=64)
+                xscl[g] = cd_pool.tile([P, 2 * WC * P], U8, name="xs", tag="xs", align_bytes=64)
+            lo, hi = (0, 2 * WC * P) if h is None else (h * WC * P, (h + 1) * WC * P)
+            nc.vector.quantize_mx(out=xcod[g][:, lo:hi].bitcast(FP8X4), scales=xscl[g][:, lo:hi], in_=xgrp[g][:, 4 * lo:4 * hi])
 
         def quant_w(g):
             cod = cd_pool.tile([P, 2 * WC * F], U32, name="wc", tag="wc", align_bytes=64)
@@ -148,10 +188,13 @@ def tile_dot_pa_kernel(tc, x_crop_bytes, x_crop_scale, W_r, W_i, b_r, b_i, out):
             nc.vector.quantize_mx(out=cod[:].bitcast(FP8X4), scales=scl[:], in_=wgrp[g][:])
             wcod[g], wscl[g] = cod, scl
 
-        def mm(g):
-            rr = acc_pool.tile([P, WC * P], F32, name="rr", tag="rr")
-            ii = acc_pool.tile([P, WC * P], F32, name="ii", tag="ii")
-            pi = acc_pool.tile([P, WC * P], F32, name="pi", tag="pi")
+        def mm(g, ws=(0, 1, 2, 3)):
+            if g not in acc:
+                rr = acc_pool.tile([P, WC * P], F32, name="rr", tag="rr")
+                ii = acc_pool.tile([P, WC * P], F32, name="ii", tag="ii")
+                pi = acc_pool.tile([P, WC * P], F32, name="pi", tag="pi")
+                acc[g] = (rr, ii, pi)
+            rr, ii, pi = acc[g]
 
             def mx(dst, w, m, c, start, stop):
                 ws_ = slice((m * WC + w) * F, (m * WC + w + 1) * F)
@@ -166,14 +209,13 @@ def tile_dot_pa_kernel(tc, x_crop_bytes, x_crop_scale, W_r, W_i, b_r, b_i, out):
                     stop=stop,
                 )
 
-            for w in range(WC):
+            for w in ws:
                 mx(ii, w, 1, 1, True, True)
-            for w in range(WC):
+            for w in ws:
                 mx(rr, w, 0, 0, True, True)
-            for w in range(WC):
+            for w in ws:
                 mx(pi, w, 0, 1, True, False)
                 mx(pi, w, 1, 0, False, True)
-            acc[g] = (rr, ii, pi)
 
         def e1t(g):
             t = ep_pool.tile([P, WC * P], F32, name="t", tag="t")
@@ -226,13 +268,106 @@ def tile_dot_pa_kernel(tc, x_crop_bytes, x_crop_scale, W_r, W_i, b_r, b_i, out):
                 in_=ots[g][:].rearrange("p (c n) -> p c n", c=2),
             )
 
-        load_x_half(0, 0)
-        load_w(0, 0)
-        load_x_half(0, 1)
-        load_w(0, 1)
-        load_x(1)
+        hacc, ht, hr, hi1, hto = {}, {}, {}, {}, {}
+
+        def mm_half(g, h):
+            if h == 0:
+                rr = acc_pool.tile([P, 2 * P], F32, name="rr", tag="rr")
+                ii = acc_pool.tile([P, 2 * P], F32, name="ii", tag="ii")
+                pi = acc_pool.tile([P, 2 * P], F32, name="pi", tag="pi")
+            else:
+                ii = tx_pool.tile([P, 2 * P], F32, name="tx", tag="tx")
+                rr = tx_pool.tile([P, 2 * P], F32, name="tx", tag="tx")
+                pi = tx_pool.tile([P, 2 * P], F32, name="tx", tag="tx")
+            hacc[h] = (rr, ii, pi)
+
+            def mx(dst, w, m, c, start, stop):
+                ws_ = slice((m * WC + w) * F, (m * WC + w + 1) * F)
+                xs_ = slice((2 * w + c) * P, (2 * w + c + 1) * P)
+                nc.tensor.matmul_mx(
+                    out=dst[:, (w - 2 * h) * P:(w - 2 * h + 1) * P],
+                    lhsT=wcod[g][:, ws_].bitcast(FP8X4),
+                    lhsT_scale=wscl[g][:, ws_],
+                    rhs=xcod[g][:, xs_].bitcast(FP8X4),
+                    rhs_scale=xscl[g][:, xs_],
+                    start=start,
+                    stop=stop,
+                )
+
+            ws = (2 * h, 2 * h + 1)
+            for w in ws:
+                mx(ii, w, 1, 1, True, True)
+            for w in ws:
+                mx(rr, w, 0, 0, True, True)
+            for w in ws:
+                mx(pi, w, 0, 1, True, False)
+                mx(pi, w, 1, 0, False, True)
+
+        def e1_half(h, rr_on_vector):
+            rr, ii, pi = hacc[h]
+            ht[h] = ep_pool.tile([P, 2 * P], F32, name="t", tag="t")
+            hr[h] = ep_pool.tile([P, 2 * P], F32, name="r1", tag="r1")
+            hi1[h] = ep_pool.tile([P, 2 * P], F32, name="i1", tag="i1")
+            nc.scalar.activation(out=ht[h][:], in_=ii[:], func=ACT.Identity, bias=brc[:], scale=-1.0)
+            if rr_on_vector:
+                nc.vector.tensor_copy(out=hr[h][:], in_=rr[:])
+            else:
+                nc.scalar.copy(out=hr[h][:], in_=rr[:])
+            nc.scalar.activation(out=hi1[h][:], in_=pi[:], func=ACT.Relu, bias=bic[:], scale=1.0)
+
+        def tout_half(h, spare):
+            if spare:
+                to = tx_pool.tile([P, 4 * F], F32, name="tx", tag="tx")
+            else:
+                to = acc_pool.tile([P, 4 * F], F32, name="to", tag="to")
+            for w in range(2):
+                nc.tensor.matmul(to[:, w * F:(w + 1) * F], lhsT=hr[h][:, w * P:(w + 1) * P], rhs=ident[:], start=True, stop=False, is_transpose=True)
+                nc.tensor.matmul(to[:, w * F:(w + 1) * F], lhsT=ht[h][:, w * P:(w + 1) * P], rhs=ident[:], start=False, stop=True, is_transpose=True)
+            for w in range(2):
+                nc.tensor.transpose(to[:, (2 + w) * F:(3 + w) * F], hi1[h][:, w * P:(w + 1) * P], ident[:])
+            hto[h] = to
+
+        def e2_half(g, h, queue):
+            o = ot_pool.tile([P, 4 * F], F32, name="ot", tag="ot")
+            nc.scalar.activation(out=o[:], in_=hto[h][:], func=ACT.Relu)
+            queue.dma_start(
+                out=out[:, :, g, 2 * h:2 * h + 2, :].rearrange("b c w f -> b c (w f)"),
+                in_=o[:].rearrange("p (c n) -> p c n", c=2),
+            )
+
+        def quants(g):
+            if QW_FIRST:
+                quant_w(g)
+                quant_x(g)
+            else:
+                quant_x(g)
+                quant_w(g)
+
+        if HEAD == 1:
+            load_x_px(0, 0, 1)
+            load_x_px(0, 1, 2)
+            load_w(0, 0)
+            load_x_px(0, 2, WC)
+            load_w(0, 1)
+        elif HEAD == 2:
+            load_x_px(0, 0, 1)
+            load_x_px(0, 1, 2)
+            load_x_px(0, 2, WC)
+            load_w(0, 0)
+            load_w(0, 1)
+        elif HEAD == 3:
+            load_x_px(0, 0, 1)
+            load_w(0, 0)
+            load_x_px(0, 1, WC)
+            load_w(0, 1)
+        else:
+            load_x_px(0, 0, 2)
+            load_w(0, 0)
+            load_x_px(0, 2, WC)
+            load_w(0, 1)
+        load_x_px(1, 0, WC)
         for g in range(2, HC):
-            load_x(g)
+            load_x_px(g, 0, WC)
             load_w(g - 1, 0)
             load_w(g - 1, 1)
         load_w(HC - 1, 0)
@@ -241,27 +376,54 @@ def tile_dot_pa_kernel(tc, x_crop_bytes, x_crop_scale, W_r, W_i, b_r, b_i, out):
         def has(g):
             return 0 <= g < HC
 
-        cast(0, 0, GW // 2, on_vector=True)
-        cast(0, GW, GW + GW // 2, on_vector=True)
-        cast(0, GW // 2, GW)
-        cast(0, GW + GW // 2, 2 * GW)
-        txp(0)
-        wil_g(0)
-        cast(1, 0, GW // 2)
-        cast(1, GW, GW + GW // 2)
-        cast(1, GW // 2, GW)
-        cast(1, GW + GW // 2, 2 * GW)
-        wil_s(0)
+        if HEAD:
+            for w in range(WC):
+                cast_px(0, w, w + 1, on_vector=(w == 0))
+            txp(0)
+            wil_g(0, (0, WC, G_UNITS[0]))
+            wpe_mm(0)
+            wil_s(0)
+            wpe_cp(0)
+            cast_px(1, 0, 2)
+            cast_px(1, 2, 4)
+        else:
+            cast_px(0, 0, 2, on_vector=True)
+            cast_px(0, 2, 4)
+            if G_UNITS[0] > WC:
+                wil_g(0, (0, WC, G_UNITS[0]))
+            else:
+                wil_g(0)
+            if PE0_AT == 0:
+                txp(0)
+                wpe_mm(0)
+            elif PE0_AT == 1:
+                txp(0, (0, 1))
+                wpe_mm(0)
+                txp(0, (2, 3))
+            else:
+                txp(0, (0, 1, 2))
+                wpe_mm(0)
+                txp(0, (3,))
+            wpe_cp(0)
+            if WS0_EARLY == 1:
+                wil_s(0)
+            cast_px(1, 0, 2)
+            if WS0_EARLY == 2:
+                wil_s(0)
+            cast_px(1, 2, 4)
+            if not WS0_EARLY:
+                wil_s(0)
         nc.scalar.copy(out=brc[:], in_=brb[:])
         nc.scalar.copy(out=bic[:], in_=bib[:])
         em(0)
         txp(1)
         last = HC - 1
         for j in range(last):
-            quant_x(j)
-            quant_w(j)
+            quants(j)
             if has(j - 1):
                 r1(j - 1)
+            if SHAKE:
+                new_xg(j + 1)
             wil_g(j + 1)
             if has(j + 2):
                 cast(j + 2, 0, GW)
@@ -272,30 +434,61 @@ def tile_dot_pa_kernel(tc, x_crop_bytes, x_crop_scale, W_r, W_i, b_r, b_i, out):
             if has(j - 1):
                 tos[j - 1] = tout(j - 1, r1s)
             e1t(j)
+            wpe_mm(j + 1)
             if has(j + 2):
                 cast(j + 2, GW, 2 * GW)
             e1i(j)
+            wpe_cp(j + 1)
             if has(j - 1):
                 e2r(j - 1)
-            em(j + 1)
+            if TAIL and j == last - 1:
+                em(last, (0, 1, 2))
+                quant_w(last)
+                quant_x(last, 0)
+                em(last, (3,))
+                if TAIL == 2:
+                    quant_x(last, 1)
+            else:
+                em(j + 1)
             if has(j + 2):
                 txp(j + 2)
             tos[j] = tout(j, i1s)
 
-        quant_x(last)
-        quant_w(last)
-        r1(last - 1)
-        e2i(last - 1)
-        tos[last - 1] = tout(last - 1, r1s)
-        mm(last)
-        e1t(last)
-        e2r(last - 1)
-        e1i(last)
-        r1(last)
-        tr_last = tout(last, r1s, spare=True)
-        ti_last = tout(last, i1s, spare=True)
-        ot = ot_pool.tile([P, 2 * WC * F], F32, name="ot", tag="ot")
-        nc.scalar.activation(out=ot[:, 0:WC * F], in_=tr_last[:], func=ACT.Relu)
-        nc.sync.dma_start(out=out[:, 0, last, :, :].rearrange("b w f -> b (w f)"), in_=ot[:, 0:WC * F])
-        nc.vector.tensor_copy(out=ot[:, WC * F:], in_=ti_last[:])
-        nc.scalar.dma_start(out=out[:, 1, last, :, :].rearrange("b w f -> b (w f)"), in_=ot[:, WC * F:])
+        if TAIL == 2:
+            r1(last - 1)
+            e2i(last - 1)
+            mm_half(last, 0)
+            tos[last - 1] = tout(last - 1, r1s)
+            e1_half(0, False)
+            e2r(last - 1)
+            tout_half(0, True)
+            mm_half(last, 1)
+            e2_half(last, 0, nc.sync)
+            e1_half(1, True)
+            tout_half(1, False)
+            e2_half(last, 1, nc.sync)
+        elif TAIL:
+            r1(last - 1)
+            quant_x(last, 1)
+            e2i(last - 1)
+            mm(last, (0, 1))
+            tos[last - 1] = tout(last - 1, r1s)
+            mm(last, (2, 3))
+        else:
+            quants(last)
+            r1(last - 1)
+            e2i(last - 1)
+            tos[last - 1] = tout(last - 1, r1s)
+            mm(last)
+        if TAIL != 2:
+            e1t(last)
+            e2r(last - 1)
+            e1i(last)
+            r1(last)
+            tr_last = tout(last, r1s, spare=True)
+            ti_last = tout(last, i1s, spare=True)
+            ot = ot_pool.tile([P, 2 * WC * F], F32, name="ot", tag="ot")
+            nc.scalar.activation(out=ot[:, 0:WC * F], in_=tr_last[:], func=ACT.Relu)
+            nc.sync.dma_start(out=out[:, 0, last, :, :].rearrange("b w f -> b (w f)"), in_=ot[:, 0:WC * F])
+            nc.vector.tensor_copy(out=ot[:, WC * F:], in_=ti_last[:])
+            nc.scalar.dma_start(out=out[:, 1, last, :, :].rearrange("b w f -> b (w f)"), in_=ot[:, WC * F:])

@@ -22,12 +22,13 @@ G_UNITS = (7, 7, 7, 7, 7, 7, 7, 5)
 PE_UNITS = (0, 0, 0, 0, 0, 0, 0, 0)
 HEAD = 0
 TAIL = 2
-SHAKE = 0
+SHAKE = 1
 QW_FIRST = 0
 XW_BUFS = 3
 IL4 = 0
 WS0_EARLY = 0
 PE0_AT = 0
+CPW_MID = 0
 
 
 def tile_dot_pa_kernel(tc, x_crop_bytes, x_crop_scale, W_r, W_i, b_r, b_i, out):
@@ -435,10 +436,18 @@ def tile_dot_pa_kernel(tc, x_crop_bytes, x_crop_scale, W_r, W_i, b_r, b_i, out):
                 tos[j - 1] = tout(j - 1, r1s)
             e1t(j)
             wpe_mm(j + 1)
-            if has(j + 2):
-                cast(j + 2, GW, 2 * GW)
-            e1i(j)
-            wpe_cp(j + 1)
+            if CPW_MID:
+                if has(j + 2):
+                    cast(j + 2, GW, GW + GW // 2)
+                wpe_cp(j + 1)
+                if has(j + 2):
+                    cast(j + 2, GW + GW // 2, 2 * GW)
+                e1i(j)
+            else:
+                if has(j + 2):
+                    cast(j + 2, GW, 2 * GW)
+                e1i(j)
+                wpe_cp(j + 1)
             if has(j - 1):
                 e2r(j - 1)
             if TAIL and j == last - 1:

@@ -19,16 +19,20 @@ FLOPS = 4 * 2 * B * HC * WC * C * F
 
 V_SUM = (5,)
 G_UNITS = (7, 7, 7, 7, 7, 7, 7, 5)
-PE_UNITS = (0, 0, 0, 0, 0, 0, 0, 0)
+PE_UNITS = (0, 1, 1, 1, 1, 1, 1, 0)
 HEAD = 0
-TAIL = 2
+TAIL = 3
 SHAKE = 1
 QW_FIRST = 0
 XW_BUFS = 3
 IL4 = 0
-WS0_EARLY = 0
+WS0_EARLY = 1
 PE0_AT = 0
-CPW_MID = 0
+CPW_MID = 1
+VCAST = 0
+OT_BUFS = 5
+QX_SPLIT = 1
+T3_ORDER = 0
 
 
 def tile_dot_pa_kernel(tc, x_crop_bytes, x_crop_scale, W_r, W_i, b_r, b_i, out):
@@ -42,7 +46,7 @@ def tile_dot_pa_kernel(tc, x_crop_bytes, x_crop_scale, W_r, W_i, b_r, b_i, out):
         wg_pool = ctx.enter_context(tc.tile_pool(name="wg_pool", bufs=1))
         cd_pool = ctx.enter_context(tc.tile_pool(name="cd_pool", bufs=2))
         ep_pool = ctx.enter_context(tc.tile_pool(name="ep_pool", bufs=2))
-        ot_pool = ctx.enter_context(tc.tile_pool(name="ot_pool", bufs=3))
+        ot_pool = ctx.enter_context(tc.tile_pool(name="ot_pool", bufs=OT_BUFS))
         tx_pool = ctx.enter_context(tc.psum_pool(name="tx_pool", bufs=4))
         acc_pool = ctx.enter_context(tc.psum_pool(name="acc_pool", bufs=1))
         ctx.enter_context(tc.manual_schedule())
@@ -336,10 +340,93 @@ def tile_dot_pa_kernel(tc, x_crop_bytes, x_crop_scale, W_r, W_i, b_r, b_i, out):
                 in_=o[:].rearrange("p (c n) -> p c n", c=2),
             )
 
+        pacc, pt, pr, pi1, pto = {}, {}, {}, {}, {}
+
+        def quant_x_px(g, w0, w1):
+            if g not in xcod:
+                xcod[g] = cd_pool.tile([P, 2 * WC * P], U32, name="xc", tag="xc", align_bytes=64)
+                xscl[g] = cd_pool.tile([P, 2 * WC * P], U8, name="xs", tag="xs", align_bytes=64)
+            lo, hi = 2 * w0 * P, 2 * w1 * P
+            nc.vector.quantize_mx(out=xcod[g][:, lo:hi].bitcast(FP8X4), scales=xscl[g][:, lo:hi], in_=xgrp[g][:, 4 * lo:4 * hi])
+
+        def mm_piece(g, ws, one_bank):
+            n = len(ws)
+            if one_bank:
+                iit = tx_pool.tile([P, n * P], F32, name="tx", tag="tx")
+                rrt = tx_pool.tile([P, n * P], F32, name="tx", tag="tx")
+                pit = tx_pool.tile([P, n * P], F32, name="tx", tag="tx")
+                ii, rr, pi = iit[:], rrt[:], pit[:]
+            else:
+                rrt = acc_pool.tile([P, n * P], F32, name="rr", tag="rr")
+                iit = acc_pool.tile([P, n * P], F32, name="ii", tag="ii")
+                pit = acc_pool.tile([P, n * P], F32, name="pi", tag="pi")
+                ii, rr, pi = iit[:], rrt[:], pit[:]
+            pacc[ws] = (rr, ii, pi)
+
+            def mx(dst, w, m, c, start, stop):
+                ws_ = slice((m * WC + w) * F, (m * WC + w + 1) * F)
+                xs_ = slice((2 * w + c) * P, (2 * w + c + 1) * P)
+                nc.tensor.matmul_mx(
+                    out=dst[:, (w - ws[0]) * P:(w - ws[0] + 1) * P],
+                    lhsT=wcod[g][:, ws_].bitcast(FP8X4),
+                    lhsT_scale=wscl[g][:, ws_],
+                    rhs=xcod[g][:, xs_].bitcast(FP8X4),
+                    rhs_scale=xscl[g][:, xs_],
+                    start=start,
+                    stop=stop,
+                )
+
+            for w in ws:
+                mx(ii, w, 1, 1, True, True)
+            for w in ws:
+                mx(rr, w, 0, 0, True, True)
+            for w in ws:
+                mx(pi, w, 0, 1, True, False)
+                mx(pi, w, 1, 0, False, True)
+
+        def e1_piece(ws, rr_on_vector):
+            n = len(ws)
+            rr, ii, pi = pacc[ws]
+            pt[ws] = ep_pool.tile([P, n * P], F32, name="t", tag="t")
+            pr[ws] = ep_pool.tile([P, n * P], F32, name="r1", tag="r1")
+            pi1[ws] = ep_pool.tile([P, n * P], F32, name="i1", tag="i1")
+            nc.scalar.activation(out=pt[ws][:], in_=ii, func=ACT.Identity, bias=brc[:], scale=-1.0)
+            if rr_on_vector:
+                nc.vector.tensor_copy(out=pr[ws][:], in_=rr)
+            else:
+                nc.scalar.copy(out=pr[ws][:], in_=rr)
+            nc.scalar.activation(out=pi1[ws][:], in_=pi, func=ACT.Relu, bias=bic[:], scale=1.0)
+
+        def tout_piece(ws, spare):
+            n = len(ws)
+            if spare:
+                to = tx_pool.tile([P, 2 * n * F], F32, name="tx", tag="tx")
+            else:
+                to = acc_pool.tile([P, 2 * n * F], F32, name="to", tag="to")
+            for w in range(n):
+                nc.tensor.matmul(to[:, w * F:(w + 1) * F], lhsT=pr[ws][:, w * P:(w + 1) * P], rhs=ident[:], start=True, stop=False, is_transpose=True)
+                nc.tensor.matmul(to[:, w * F:(w + 1) * F], lhsT=pt[ws][:, w * P:(w + 1) * P], rhs=ident[:], start=False, stop=True, is_transpose=True)
+            for w in range(n):
+                nc.tensor.transpose(to[:, (n + w) * F:(n + w + 1) * F], pi1[ws][:, w * P:(w + 1) * P], ident[:])
+            pto[ws] = to
+
+        def e2_piece(g, ws, queue):
+            n = len(ws)
+            o = ot_pool.tile([P, 2 * n * F], F32, name="ot", tag="ot")
+            nc.scalar.activation(out=o[:], in_=pto[ws][:], func=ACT.Relu)
+            queue.dma_start(
+                out=out[:, :, g, ws[0]:ws[0] + n, :].rearrange("b c w f -> b c (w f)"),
+                in_=o[:].rearrange("p (c n) -> p c n", c=2),
+            )
+
         def quants(g):
             if QW_FIRST:
                 quant_w(g)
                 quant_x(g)
+            elif QX_SPLIT:
+                quant_x(g, 0)
+                quant_x(g, 1)
+                quant_w(g)
             else:
                 quant_x(g)
                 quant_w(g)
@@ -420,6 +507,8 @@ def tile_dot_pa_kernel(tc, x_crop_bytes, x_crop_scale, W_r, W_i, b_r, b_i, out):
         txp(1)
         last = HC - 1
         for j in range(last):
+            if VCAST and has(j + 2):
+                cast(j + 2, 2 * GW - VCAST, 2 * GW, on_vector=True)
             quants(j)
             if has(j - 1):
                 r1(j - 1)
@@ -441,16 +530,23 @@ def tile_dot_pa_kernel(tc, x_crop_bytes, x_crop_scale, W_r, W_i, b_r, b_i, out):
                     cast(j + 2, GW, GW + GW // 2)
                 wpe_cp(j + 1)
                 if has(j + 2):
-                    cast(j + 2, GW + GW // 2, 2 * GW)
+                    cast(j + 2, GW + GW // 2, 2 * GW - VCAST)
                 e1i(j)
             else:
                 if has(j + 2):
-                    cast(j + 2, GW, 2 * GW)
+                    cast(j + 2, GW, 2 * GW - VCAST)
                 e1i(j)
                 wpe_cp(j + 1)
             if has(j - 1):
                 e2r(j - 1)
-            if TAIL and j == last - 1:
+            if TAIL == 3 and j == last - 1:
+                em(last, (0, 1, 2))
+                quant_w(last)
+                quant_x_px(last, 0, 2)
+                quant_x_px(last, 2, 3)
+                em(last, (3,))
+                quant_x_px(last, 3, 4)
+            elif TAIL and j == last - 1:
                 em(last, (0, 1, 2))
                 quant_w(last)
                 quant_x(last, 0)
@@ -463,7 +559,34 @@ def tile_dot_pa_kernel(tc, x_crop_bytes, x_crop_scale, W_r, W_i, b_r, b_i, out):
                 txp(j + 2)
             tos[j] = tout(j, i1s)
 
-        if TAIL == 2:
+        if TAIL == 3:
+            pa, pb, pc = (0, 1), (2,), (3,)
+            r1(last - 1)
+            e2i(last - 1)
+            mm_piece(last, pa, False)
+            tos[last - 1] = tout(last - 1, r1s)
+            e1_piece(pa, False)
+            mm_piece(last, pb, True)
+            e2r(last - 1)
+            if T3_ORDER == 0:
+                tout_piece(pa, True)
+                e1_piece(pb, False)
+                mm_piece(last, pc, False)
+                e2_piece(last, pa, nc.sync)
+                tout_piece(pb, False)
+                e1_piece(pc, True)
+                e2_piece(last, pb, nc.sync)
+            else:
+                e1_piece(pb, False)
+                mm_piece(last, pc, False)
+                tout_piece(pa, True)
+                tout_piece(pb, False)
+                e1_piece(pc, True)
+                e2_piece(last, pa, nc.sync)
+                e2_piece(last, pb, nc.sync)
+            tout_piece(pc, True)
+            e2_piece(last, pc, nc.sync)
+        elif TAIL == 2:
             r1(last - 1)
             e2i(last - 1)
             mm_half(last, 0)
@@ -489,7 +612,7 @@ def tile_dot_pa_kernel(tc, x_crop_bytes, x_crop_scale, W_r, W_i, b_r, b_i, out):
             e2i(last - 1)
             tos[last - 1] = tout(last - 1, r1s)
             mm(last)
-        if TAIL != 2:
+        if TAIL < 2:
             e1t(last)
             e2r(last - 1)
             e1i(last)

@@ -22,7 +22,7 @@ G_UNITS = (7, 7, 7, 7, 7, 7, 7, 5)
 PE_UNITS = (0, 1, 1, 1, 1, 1, 1, 0)
 HEAD = 0
 TAIL = 3
-SHAKE = 1
+SHAKE = 0
 QW_FIRST = 0
 XW_BUFS = 3
 IL4 = 0
@@ -31,8 +31,10 @@ PE0_AT = 0
 CPW_MID = 1
 VCAST = 0
 OT_BUFS = 5
-QX_SPLIT = 1
+QX_SPLIT = 2
 T3_ORDER = 0
+E2V = 0
+FINE0 = 0
 
 
 def tile_dot_pa_kernel(tc, x_crop_bytes, x_crop_scale, W_r, W_i, b_r, b_i, out):
@@ -89,6 +91,12 @@ def tile_dot_pa_kernel(tc, x_crop_bytes, x_crop_scale, W_r, W_i, b_r, b_i, out):
                 wraw[g] = wr_pool.tile([P, 2, WC, 4 * F], BF16, name="wraw", tag="wraw")
             src = (W_r, W_i)[m]
             nc.sync.dma_start(out=wraw[g][:, m], in_=src[g].rearrange("w (p j) f -> p w (j f)", j=4))
+
+        def load_w_px(g, m, w0, w1):
+            if g not in wraw:
+                wraw[g] = wr_pool.tile([P, 2, WC, 4 * F], BF16, name="wraw", tag="wraw")
+            src = (W_r, W_i)[m]
+            nc.sync.dma_start(out=wraw[g][:, m, w0:w1], in_=src[g, w0:w1].rearrange("w (p j) f -> p w (j f)", j=4))
 
         def cast(g, lo, hi, on_vector=False):
             if g not in xwide:
@@ -410,10 +418,13 @@ def tile_dot_pa_kernel(tc, x_crop_bytes, x_crop_scale, W_r, W_i, b_r, b_i, out):
                 nc.tensor.transpose(to[:, (n + w) * F:(n + w + 1) * F], pi1[ws][:, w * P:(w + 1) * P], ident[:])
             pto[ws] = to
 
-        def e2_piece(g, ws, queue):
+        def e2_piece(g, ws, queue, on_vector=False):
             n = len(ws)
             o = ot_pool.tile([P, 2 * n * F], F32, name="ot", tag="ot")
-            nc.scalar.activation(out=o[:], in_=pto[ws][:], func=ACT.Relu)
+            if on_vector:
+                nc.vector.tensor_scalar_max(out=o[:], in0=pto[ws][:], scalar1=0.0)
+            else:
+                nc.scalar.activation(out=o[:], in_=pto[ws][:], func=ACT.Relu)
             queue.dma_start(
                 out=out[:, :, g, ws[0]:ws[0] + n, :].rearrange("b c w f -> b c (w f)"),
                 in_=o[:].rearrange("p (c n) -> p c n", c=2),
@@ -423,6 +434,10 @@ def tile_dot_pa_kernel(tc, x_crop_bytes, x_crop_scale, W_r, W_i, b_r, b_i, out):
             if QW_FIRST:
                 quant_w(g)
                 quant_x(g)
+            elif QX_SPLIT == 2:
+                quant_x(g, 0)
+                quant_w(g)
+                quant_x(g, 1)
             elif QX_SPLIT:
                 quant_x(g, 0)
                 quant_x(g, 1)
@@ -448,6 +463,25 @@ def tile_dot_pa_kernel(tc, x_crop_bytes, x_crop_scale, W_r, W_i, b_r, b_i, out):
             load_w(0, 0)
             load_x_px(0, 1, WC)
             load_w(0, 1)
+        elif FINE0 == 1:
+            load_x_px(0, 0, 2)
+            load_w_px(0, 0, 0, 2)
+            load_x_px(0, 2, WC)
+            load_w_px(0, 0, 2, 4)
+            load_w(0, 1)
+        elif FINE0 == 3:
+            load_x_px(0, 0, 2)
+            load_x_px(0, 2, WC)
+            load_w_px(0, 0, 0, 2)
+            load_w_px(0, 0, 2, 4)
+            load_w(0, 1)
+        elif FINE0 == 2:
+            load_x_px(0, 0, 2)
+            load_w_px(0, 0, 0, 2)
+            load_x_px(0, 2, WC)
+            load_w_px(0, 0, 2, 4)
+            load_w_px(0, 1, 0, 2)
+            load_w_px(0, 1, 2, 4)
         else:
             load_x_px(0, 0, 2)
             load_w(0, 0)
@@ -477,7 +511,11 @@ def tile_dot_pa_kernel(tc, x_crop_bytes, x_crop_scale, W_r, W_i, b_r, b_i, out):
         else:
             cast_px(0, 0, 2, on_vector=True)
             cast_px(0, 2, 4)
-            if G_UNITS[0] > WC:
+            if FINE0 in (1, 3):
+                wil_g(0, (0, 2, WC, G_UNITS[0]))
+            elif FINE0 == 2:
+                wil_g(0, (0, 2, WC, 6, G_UNITS[0]))
+            elif G_UNITS[0] > WC:
                 wil_g(0, (0, WC, G_UNITS[0]))
             else:
                 wil_g(0)
@@ -572,10 +610,10 @@ def tile_dot_pa_kernel(tc, x_crop_bytes, x_crop_scale, W_r, W_i, b_r, b_i, out):
                 tout_piece(pa, True)
                 e1_piece(pb, False)
                 mm_piece(last, pc, False)
-                e2_piece(last, pa, nc.sync)
+                e2_piece(last, pa, nc.sync, E2V >= 1)
                 tout_piece(pb, False)
-                e1_piece(pc, True)
-                e2_piece(last, pb, nc.sync)
+                e1_piece(pc, E2V < 2)
+                e2_piece(last, pb, nc.sync, E2V >= 2)
             else:
                 e1_piece(pb, False)
                 mm_piece(last, pc, False)

@@ -17,9 +17,9 @@ P = 128
 GW = WC * C
 FLOPS = 4 * 2 * B * HC * WC * C * F
 
-V_SUM = (5,)
-G_UNITS = (7, 7, 7, 7, 7, 7, 7, 5)
-PE_UNITS = (0, 1, 1, 1, 1, 1, 1, 0)
+V_SUM = ()
+G_UNITS = (7, 6, 6, 6, 6, 6, 6, 5)
+PE_UNITS = (0, 0, 0, 0, 0, 0, 0, 0)
 HEAD = 0
 TAIL = 3
 SHAKE = 0
@@ -28,13 +28,17 @@ XW_BUFS = 3
 IL4 = 0
 WS0_EARLY = 1
 PE0_AT = 0
-CPW_MID = 1
+CPW_MID = 0
 VCAST = 0
 OT_BUFS = 5
 QX_SPLIT = 2
 T3_ORDER = 0
 E2V = 0
 FINE0 = 0
+E2N = (0, 1, 1, 1, 1, 1, 1)
+EP_BUFS = 2
+S0_AHEAD = 0
+VHEAD = 0
 
 
 def tile_dot_pa_kernel(tc, x_crop_bytes, x_crop_scale, W_r, W_i, b_r, b_i, out):
@@ -47,7 +51,7 @@ def tile_dot_pa_kernel(tc, x_crop_bytes, x_crop_scale, W_r, W_i, b_r, b_i, out):
         xg_pool = ctx.enter_context(tc.tile_pool(name="xg_pool", bufs=3 if SHAKE else 2))
         wg_pool = ctx.enter_context(tc.tile_pool(name="wg_pool", bufs=1))
         cd_pool = ctx.enter_context(tc.tile_pool(name="cd_pool", bufs=2))
-        ep_pool = ctx.enter_context(tc.tile_pool(name="ep_pool", bufs=2))
+        ep_pool = ctx.enter_context(tc.tile_pool(name="ep_pool", bufs=EP_BUFS))
         ot_pool = ctx.enter_context(tc.tile_pool(name="ot_pool", bufs=OT_BUFS))
         tx_pool = ctx.enter_context(tc.psum_pool(name="tx_pool", bufs=4))
         acc_pool = ctx.enter_context(tc.psum_pool(name="acc_pool", bufs=1))
@@ -141,8 +145,8 @@ def tile_dot_pa_kernel(tc, x_crop_bytes, x_crop_scale, W_r, W_i, b_r, b_i, out):
                     op=ALU.mult,
                 )
 
-        def il_views(g, u0, u1):
-            if IL4:
+        def il_views(g, u0, u1, il4=False):
+            if il4:
                 dst = wgrp[g][:, u0 * C:u1 * C].rearrange("p (w c i j) -> p w c j i", w=u1 - u0, j=4, i=4)
                 src = wraw[g][:].rearrange("p m w n -> p (m w) n")[:, u0:u1, :].rearrange("p w (j c i) -> p w c j i", j=4, i=4)
                 return dst, src
@@ -161,13 +165,13 @@ def tile_dot_pa_kernel(tc, x_crop_bytes, x_crop_scale, W_r, W_i, b_r, b_i, out):
                 new_wg(g)
             cuts = cuts or (0, G_UNITS[g])
             for a, b_ in zip(cuts[:-1], cuts[1:]):
-                dst, src = il_views(g, a, b_)
+                dst, src = il_views(g, a, b_, IL4 >= 1)
                 nc.gpsimd.tensor_scalar(out=dst, in0=src, scalar1=1.0, scalar2=0.0, op0=ALU.mult, op1=ALU.add)
 
         def wil_s(g):
             u0 = G_UNITS[g] + PE_UNITS[g]
             if u0 < 8:
-                dst, src = il_views(g, u0, 8)
+                dst, src = il_views(g, u0, 8, IL4 >= 2)
                 nc.scalar.copy(out=dst, in_=src)
 
         def wpe_mm(g, tags=("ii", "rr")):
@@ -469,6 +473,14 @@ def tile_dot_pa_kernel(tc, x_crop_bytes, x_crop_scale, W_r, W_i, b_r, b_i, out):
             load_x_px(0, 2, WC)
             load_w_px(0, 0, 2, 4)
             load_w(0, 1)
+        elif FINE0 == 4:
+            load_x_px(0, 0, 2)
+            load_x_px(0, 2, WC)
+            load_w_px(0, 0, 0, 2)
+            load_x_px(1, 0, 2)
+            load_w_px(0, 0, 2, 4)
+            load_x_px(1, 2, WC)
+            load_w(0, 1)
         elif FINE0 == 3:
             load_x_px(0, 0, 2)
             load_x_px(0, 2, WC)
@@ -487,7 +499,8 @@ def tile_dot_pa_kernel(tc, x_crop_bytes, x_crop_scale, W_r, W_i, b_r, b_i, out):
             load_w(0, 0)
             load_x_px(0, 2, WC)
             load_w(0, 1)
-        load_x_px(1, 0, WC)
+        if FINE0 != 4:
+            load_x_px(1, 0, WC)
         for g in range(2, HC):
             load_x_px(g, 0, WC)
             load_w(g - 1, 0)
@@ -509,9 +522,10 @@ def tile_dot_pa_kernel(tc, x_crop_bytes, x_crop_scale, W_r, W_i, b_r, b_i, out):
             cast_px(1, 0, 2)
             cast_px(1, 2, 4)
         else:
-            cast_px(0, 0, 2, on_vector=True)
-            cast_px(0, 2, 4)
-            if FINE0 in (1, 3):
+            cast_px(0, 0, 2, on_vector=(VHEAD >= 0))
+            cast(0, 2 * C, 4 * C, VHEAD >= 1)
+            cast(0, GW + 2 * C, GW + 4 * C, VHEAD >= 2)
+            if FINE0 in (1, 3, 4):
                 wil_g(0, (0, 2, WC, G_UNITS[0]))
             elif FINE0 == 2:
                 wil_g(0, (0, 2, WC, 6, G_UNITS[0]))
@@ -544,6 +558,7 @@ def tile_dot_pa_kernel(tc, x_crop_bytes, x_crop_scale, W_r, W_i, b_r, b_i, out):
         em(0)
         txp(1)
         last = HC - 1
+        st2 = {"cur": -1, "next": 0}
         for j in range(last):
             if VCAST and has(j + 2):
                 cast(j + 2, 2 * GW - VCAST, 2 * GW, on_vector=True)
@@ -556,14 +571,25 @@ def tile_dot_pa_kernel(tc, x_crop_bytes, x_crop_scale, W_r, W_i, b_r, b_i, out):
             if has(j + 2):
                 cast(j + 2, 0, GW)
             wil_s(j + 1)
-            if has(j - 1):
-                e2i(j - 1)
+            ge = st2["cur"] if E2N[j] else -1
+            if ge >= 0:
+                e2i(ge)
             mm(j)
-            if has(j - 1):
-                tos[j - 1] = tout(j - 1, r1s)
-            e1t(j)
-            wpe_mm(j + 1)
-            if CPW_MID:
+            if ge >= 0:
+                tos[ge] = tout(ge, r1s)
+            if S0_AHEAD and j == 0:
+                wpe_mm(1, ("to",))
+                cast(2, GW, GW + GW // 2)
+                wpe_cp(1)
+                cast(2, GW + GW // 2, 2 * GW - VCAST)
+                e1t(0)
+                e1i(0)
+            else:
+                e1t(j)
+                wpe_mm(j + 1)
+            if S0_AHEAD and j == 0:
+                pass
+            elif CPW_MID:
                 if has(j + 2):
                     cast(j + 2, GW, GW + GW // 2)
                 wpe_cp(j + 1)
@@ -575,8 +601,17 @@ def tile_dot_pa_kernel(tc, x_crop_bytes, x_crop_scale, W_r, W_i, b_r, b_i, out):
                     cast(j + 2, GW, 2 * GW - VCAST)
                 e1i(j)
                 wpe_cp(j + 1)
-            if has(j - 1):
-                e2r(j - 1)
+            if ge >= 0:
+                e2r(ge)
+                st2["cur"] = -1
+                st2["next"] = ge + 1
+            for extra in range(E2N[j] - 1):
+                gx = st2["next"]
+                tos[gx] = tout(gx, i1s)
+                e2i(gx)
+                tos[gx] = tout(gx, r1s)
+                e2r(gx)
+                st2["next"] = gx + 1
             if TAIL == 3 and j == last - 1:
                 em(last, (0, 1, 2))
                 quant_w(last)
@@ -595,7 +630,10 @@ def tile_dot_pa_kernel(tc, x_crop_bytes, x_crop_scale, W_r, W_i, b_r, b_i, out):
                 em(j + 1)
             if has(j + 2):
                 txp(j + 2)
-            tos[j] = tout(j, i1s)
+            if st2["cur"] < 0:
+                gn = st2["next"]
+                tos[gn] = tout(gn, i1s)
+                st2["cur"] = gn
 
         if TAIL == 3:
             pa, pb, pc = (0, 1), (2,), (3,)

@@ -18,8 +18,8 @@ GW = WC * C
 FLOPS = 4 * 2 * B * HC * WC * C * F
 
 V_SUM = ()
-G_UNITS = (7, 6, 6, 6, 6, 6, 6, 5)
-PE_UNITS = (0, 0, 0, 0, 0, 0, 0, 0)
+G_UNITS = (6, 6, 6, 6, 6, 6, 6, 5)
+PE_UNITS = (0, 1, 1, 1, 1, 1, 1, 0)
 HEAD = 0
 TAIL = 3
 SHAKE = 0
@@ -28,17 +28,18 @@ XW_BUFS = 3
 IL4 = 0
 WS0_EARLY = 1
 PE0_AT = 0
-CPW_MID = 0
+CPW_MID = 1
 VCAST = 0
 OT_BUFS = 5
 QX_SPLIT = 2
 T3_ORDER = 0
 E2V = 0
-FINE0 = 0
+FINE0 = 5
 E2N = (0, 1, 1, 1, 1, 1, 1)
 EP_BUFS = 2
 S0_AHEAD = 0
 VHEAD = 0
+WX_ORDER = 1
 
 
 def tile_dot_pa_kernel(tc, x_crop_bytes, x_crop_scale, W_r, W_i, b_r, b_i, out):
@@ -473,6 +474,20 @@ def tile_dot_pa_kernel(tc, x_crop_bytes, x_crop_scale, W_r, W_i, b_r, b_i, out):
             load_x_px(0, 2, WC)
             load_w_px(0, 0, 2, 4)
             load_w(0, 1)
+        elif FINE0 == 5:
+            load_x_px(0, 0, 1)
+            load_x_px(0, 1, 2)
+            load_w_px(0, 0, 0, 2)
+            load_x_px(0, 2, WC)
+            load_w_px(0, 0, 2, 4)
+            load_w(0, 1)
+        elif FINE0 == 6:
+            load_x_px(0, 0, 1)
+            load_w_px(0, 0, 0, 2)
+            load_x_px(0, 1, 2)
+            load_x_px(0, 2, WC)
+            load_w_px(0, 0, 2, 4)
+            load_w(0, 1)
         elif FINE0 == 4:
             load_x_px(0, 0, 2)
             load_x_px(0, 2, WC)
@@ -502,9 +517,12 @@ def tile_dot_pa_kernel(tc, x_crop_bytes, x_crop_scale, W_r, W_i, b_r, b_i, out):
         if FINE0 != 4:
             load_x_px(1, 0, WC)
         for g in range(2, HC):
-            load_x_px(g, 0, WC)
+            if not WX_ORDER:
+                load_x_px(g, 0, WC)
             load_w(g - 1, 0)
             load_w(g - 1, 1)
+            if WX_ORDER:
+                load_x_px(g, 0, WC)
         load_w(HC - 1, 0)
         load_w(HC - 1, 1)
 
@@ -522,10 +540,15 @@ def tile_dot_pa_kernel(tc, x_crop_bytes, x_crop_scale, W_r, W_i, b_r, b_i, out):
             cast_px(1, 0, 2)
             cast_px(1, 2, 4)
         else:
-            cast_px(0, 0, 2, on_vector=(VHEAD >= 0))
-            cast(0, 2 * C, 4 * C, VHEAD >= 1)
-            cast(0, GW + 2 * C, GW + 4 * C, VHEAD >= 2)
-            if FINE0 in (1, 3, 4):
+            if FINE0 in (5, 6):
+                cast_px(0, 0, 1, on_vector=True)
+                cast_px(0, 1, 2)
+                cast_px(0, 2, 4)
+            else:
+                cast_px(0, 0, 2, on_vector=(VHEAD >= 0))
+                cast(0, 2 * C, 4 * C, VHEAD >= 1)
+                cast(0, GW + 2 * C, GW + 4 * C, VHEAD >= 2)
+            if FINE0 in (1, 3, 4, 5, 6):
                 wil_g(0, (0, 2, WC, G_UNITS[0]))
             elif FINE0 == 2:
                 wil_g(0, (0, 2, WC, 6, G_UNITS[0]))
@@ -639,6 +662,37 @@ def tile_dot_pa_kernel(tc, x_crop_bytes, x_crop_scale, W_r, W_i, b_r, b_i, out):
             pa, pb, pc = (0, 1), (2,), (3,)
             r1(last - 1)
             e2i(last - 1)
+        if TAIL == 3 and T3_ORDER == 2:
+            mm_piece(last, pa, False)
+            mm_piece(last, pb, True)
+            tos[last - 1] = tout(last - 1, r1s)
+            e1_piece(pa, False)
+            e2r(last - 1)
+            e1_piece(pb, False)
+            mm_piece(last, pc, False)
+            tout_piece(pa, True)
+            e1_piece(pc, True)
+            tout_piece(pb, False)
+            tout_piece(pc, True)
+            e2_piece(last, pa, nc.sync, True)
+            e2_piece(last, pb, nc.sync, True)
+            e2_piece(last, pc, nc.sync)
+        elif TAIL == 3 and T3_ORDER == 3:
+            mm_piece(last, pa, False)
+            mm_piece(last, pb, True)
+            e1_piece(pa, False)
+            tos[last - 1] = tout(last - 1, r1s)
+            e1_piece(pb, False)
+            mm_piece(last, pc, False)
+            e2r(last - 1)
+            tout_piece(pa, True)
+            e1_piece(pc, True)
+            tout_piece(pb, False)
+            tout_piece(pc, True)
+            e2_piece(last, pa, nc.sync, True)
+            e2_piece(last, pb, nc.sync, True)
+            e2_piece(last, pc, nc.sync)
+        elif TAIL == 3:
             mm_piece(last, pa, False)
             tos[last - 1] = tout(last - 1, r1s)
             e1_piece(pa, False)

@@ -17,29 +17,17 @@ P = 128
 GW = WC * C
 FLOPS = 4 * 2 * B * HC * WC * C * F
 
-V_SUM = ()
 G_UNITS = (6, 6, 6, 6, 6, 6, 6, 5)
 PE_UNITS = (0, 1, 1, 1, 1, 1, 1, 0)
-HEAD = 0
-TAIL = 3
-SHAKE = 0
 QW_FIRST = 0
-XW_BUFS = 3
-IL4 = 0
-WS0_EARLY = 1
-PE0_AT = 0
-CPW_MID = 1
-VCAST = 0
-OT_BUFS = 5
-QX_SPLIT = 2
-T3_ORDER = 0
-E2V = 0
-FINE0 = 5
-E2N = (0, 1, 1, 1, 1, 1, 1)
-EP_BUFS = 2
-S0_AHEAD = 0
-VHEAD = 0
-WX_ORDER = 1
+NEW_TAIL = 1
+TV = 1
+WS_FIRST = ()
+P_EM = {}
+P_AT = 0
+NEW_HEAD = 0
+WARM_PE = 0
+LATE_BIAS = 0
 
 
 def tile_dot_pa_kernel(tc, x_crop_bytes, x_crop_scale, W_r, W_i, b_r, b_i, out):
@@ -48,19 +36,22 @@ def tile_dot_pa_kernel(tc, x_crop_bytes, x_crop_scale, W_r, W_i, b_r, b_i, out):
         const = ctx.enter_context(tc.tile_pool(name="const", bufs=1))
         xb_pool = ctx.enter_context(tc.tile_pool(name="xb_pool", bufs=HC))
         wr_pool = ctx.enter_context(tc.tile_pool(name="wr_pool", bufs=HC))
-        xw_pool = ctx.enter_context(tc.tile_pool(name="xw_pool", bufs=XW_BUFS))
-        xg_pool = ctx.enter_context(tc.tile_pool(name="xg_pool", bufs=3 if SHAKE else 2))
+        xw_pool = ctx.enter_context(tc.tile_pool(name="xw_pool", bufs=3))
+        xg_pool = ctx.enter_context(tc.tile_pool(name="xg_pool", bufs=2))
         wg_pool = ctx.enter_context(tc.tile_pool(name="wg_pool", bufs=1))
         cd_pool = ctx.enter_context(tc.tile_pool(name="cd_pool", bufs=2))
-        ep_pool = ctx.enter_context(tc.tile_pool(name="ep_pool", bufs=EP_BUFS))
-        ot_pool = ctx.enter_context(tc.tile_pool(name="ot_pool", bufs=OT_BUFS))
-        tx_pool = ctx.enter_context(tc.psum_pool(name="tx_pool", bufs=4))
-        acc_pool = ctx.enter_context(tc.psum_pool(name="acc_pool", bufs=1))
+        ep_pool = ctx.enter_context(tc.tile_pool(name="ep_pool", bufs=2))
+        ot_pool = ctx.enter_context(tc.tile_pool(name="ot_pool", bufs=5))
+        pl_pool = ctx.enter_context(tc.tile_pool(name="pl_pool", bufs=1))
+        ps_pool = ctx.enter_context(tc.psum_pool(name="ps_pool", bufs=1))
         ctx.enter_context(tc.manual_schedule())
 
         xbytes, wraw, xwide, xgrp, wgrp, txs, wps = {}, {}, {}, {}, {}, {}, {}
         xcod, xscl, wcod, wscl = {}, {}, {}, {}
         acc, tt, r1s, i1s, tos, ots = {}, {}, {}, {}, {}, {}
+
+        def bank(tag, cols, dt=F32):
+            return ps_pool.tile([P, cols], dt, name=tag, tag=tag)
 
         sct = const.tile([P, 1, 2, 2], F32, name="sct", tag="sct")
         nc.scalar.dma_start(
@@ -69,13 +60,17 @@ def tile_dot_pa_kernel(tc, x_crop_bytes, x_crop_scale, W_r, W_i, b_r, b_i, out):
         )
         brb = const.tile([P, 1], BF16, name="brb", tag="brb")
         bib = const.tile([P, 1], BF16, name="bib", tag="bib")
-        nc.scalar.dma_start(out=brb[:], in_=b_r.rearrange("(f o) -> f o", o=1))
-        nc.scalar.dma_start(out=bib[:], in_=b_i.rearrange("(f o) -> f o", o=1))
+
+        def load_bias():
+            nc.scalar.dma_start(out=brb[:], in_=b_r.rearrange("(f o) -> f o", o=1))
+            nc.scalar.dma_start(out=bib[:], in_=b_i.rearrange("(f o) -> f o", o=1))
+
+        if not LATE_BIAS:
+            load_bias()
         ident = const.tile([P, P], F32, name="ident", tag="ident")
         make_identity(nc, ident[:])
-        if sum(PE_UNITS):
-            identb = const.tile([P, P], BF16, name="identb", tag="identb")
-            nc.vector.tensor_copy(out=identb[:], in_=ident[:])
+        identb = const.tile([P, P], BF16, name="identb", tag="identb")
+        nc.vector.tensor_copy(out=identb[:], in_=ident[:])
         warm = const.tile([P, 1], F32, name="warm", tag="warm")
         warm2 = const.tile([P, 1], F32, name="warm2", tag="warm2")
         nc.gpsimd.memset(warm[:], 0.0)
@@ -83,21 +78,15 @@ def tile_dot_pa_kernel(tc, x_crop_bytes, x_crop_scale, W_r, W_i, b_r, b_i, out):
         brc = const.tile([P, 1], F32, name="brc", tag="brc")
         bic = const.tile([P, 1], F32, name="bic", tag="bic")
 
-        def load_x_px(g, w0, w1):
-            if w0 == 0:
+        def load_x(g, w0, w1):
+            if g not in xbytes:
                 xbytes[g] = xb_pool.tile([P, 2 * GW], U8, name="xbytes", tag="xbytes")
             nc.sync.dma_start(
                 out=xbytes[g][:].rearrange("p (c n) -> p c n", c=2)[:, :, w0 * C:w1 * C],
                 in_=x_crop_bytes[:, :, g, w0:w1, :].rearrange("b c w k -> b c (w k)"),
             )
 
-        def load_w(g, m):
-            if m == 0:
-                wraw[g] = wr_pool.tile([P, 2, WC, 4 * F], BF16, name="wraw", tag="wraw")
-            src = (W_r, W_i)[m]
-            nc.sync.dma_start(out=wraw[g][:, m], in_=src[g].rearrange("w (p j) f -> p w (j f)", j=4))
-
-        def load_w_px(g, m, w0, w1):
+        def load_w(g, m, w0=0, w1=WC):
             if g not in wraw:
                 wraw[g] = wr_pool.tile([P, 2, WC, 4 * F], BF16, name="wraw", tag="wraw")
             src = (W_r, W_i)[m]
@@ -120,7 +109,7 @@ def tile_dot_pa_kernel(tc, x_crop_bytes, x_crop_scale, W_r, W_i, b_r, b_i, out):
         def txp(g, ws=(0, 1, 2, 3)):
             words = xwide[g][:].bitcast(F32)
             for w in ws:
-                tx = tx_pool.tile([P, 4 * P], F32, name="tx", tag="tx")
+                tx = bank("tx%d" % w, 4 * P)
                 for u in range(2):
                     for c in range(2):
                         off = (c * WC + w) * (C // 2)
@@ -132,13 +121,15 @@ def tile_dot_pa_kernel(tc, x_crop_bytes, x_crop_scale, W_r, W_i, b_r, b_i, out):
                 txs[g, w] = tx
 
         def new_xg(g):
-            xgrp[g] = xg_pool.tile([P, 2 * GW], BF16, name="xg", tag="xg", align_bytes=64)
+            if g not in xgrp:
+                xgrp[g] = xg_pool.tile([P, 2 * GW], BF16, name="xg", tag="xg", align_bytes=64)
 
         def em(g, ws=(0, 1, 2, 3)):
-            if g not in xgrp:
-                new_xg(g)
+            new_xg(g)
             xg = xgrp[g]
             for w in ws:
+                if w in P_EM.get(g, ()):
+                    continue
                 nc.vector.tensor_tensor(
                     out=xg[:, w * 2 * C:(w + 1) * 2 * C].rearrange("p (n u e) -> p n u e", u=2, e=2),
                     in0=txs[g, w][:].bitcast(BF16).rearrange("p (u n e) -> p n u e", u=2, e=2),
@@ -146,58 +137,75 @@ def tile_dot_pa_kernel(tc, x_crop_bytes, x_crop_scale, W_r, W_i, b_r, b_i, out):
                     op=ALU.mult,
                 )
 
-        def il_views(g, u0, u1, il4=False):
-            if il4:
-                dst = wgrp[g][:, u0 * C:u1 * C].rearrange("p (w c i j) -> p w c j i", w=u1 - u0, j=4, i=4)
-                src = wraw[g][:].rearrange("p m w n -> p (m w) n")[:, u0:u1, :].rearrange("p w (j c i) -> p w c j i", j=4, i=4)
-                return dst, src
+        xpl, xpp = {}, {}
+
+        def em_p_planes(g):
+            for w in P_EM.get(g, ()):
+                xpl[g, w] = pl_pool.tile([P, 4, 2 * P], BF16, name="xpl", tag="xpl")
+                for t in range(4):
+                    nc.scalar.activation(
+                        out=xpl[g, w][:, t, :],
+                        in_=txs[g, w][:].bitcast(BF16).rearrange("p (u n e) -> p u n e", u=2, e=2)[:, t // 2, :, t % 2],
+                        func=ACT.Copy,
+                        scale=sct[:].rearrange("p o u e -> p (o u e)")[:, t:t + 1],
+                    )
+
+        def em_p_mm(g):
+            for w in P_EM.get(g, ()):
+                xpp[g, w] = bank("rr", 2 * C, BF16)
+                for h in range(2):
+                    nc.tensor.matmul(
+                        xpp[g, w][:, h * C:(h + 1) * C], lhsT=identb[:],
+                        rhs=xpl[g, w][:, :, h * P:(h + 1) * P].rearrange("p t n -> p n t"),
+                        start=True, stop=True,
+                    )
+
+        def em_p_cp(g):
+            for w in P_EM.get(g, ()):
+                nc.scalar.copy(out=xgrp[g][:, w * 2 * C:(w + 1) * 2 * C], in_=xpp[g, w][:])
+
+        def il_views(g, u0, u1):
             dst = wgrp[g][:, u0 * C:u1 * C].rearrange("p (w f j) -> p w f j", w=u1 - u0, j=4)
             src = wraw[g][:].rearrange("p m w n -> p (m w) n")[:, u0:u1, :].rearrange("p w (j f) -> p w f j", j=4)
             return dst, src
 
-        def new_wg(g):
-            if SHAKE:
-                wgrp[g] = xg_pool.tile([P, 2 * GW], BF16, name="xg", tag="xg", align_bytes=64)
-            else:
-                wgrp[g] = wg_pool.tile([P, 2 * GW], BF16, name="wg", tag="wg", align_bytes=64)
-
         def wil_g(g, cuts=None):
             if g not in wgrp:
-                new_wg(g)
+                wgrp[g] = wg_pool.tile([P, 2 * GW], BF16, name="wg", tag="wg", align_bytes=64)
             cuts = cuts or (0, G_UNITS[g])
             for a, b_ in zip(cuts[:-1], cuts[1:]):
-                dst, src = il_views(g, a, b_, IL4 >= 1)
+                dst, src = il_views(g, a, b_)
                 nc.gpsimd.tensor_scalar(out=dst, in0=src, scalar1=1.0, scalar2=0.0, op0=ALU.mult, op1=ALU.add)
 
         def wil_s(g):
             u0 = G_UNITS[g] + PE_UNITS[g]
             if u0 < 8:
-                dst, src = il_views(g, u0, 8, IL4 >= 2)
+                dst, src = il_views(g, u0, 8)
                 nc.scalar.copy(out=dst, in_=src)
 
-        def wpe_mm(g, tags=("ii", "rr")):
-            wps[g] = []
-            for k in range(0, PE_UNITS[g], 2):
-                n = min(2, PE_UNITS[g] - k)
-                wp = acc_pool.tile([P, n * C], BF16, name="wp", tag=tags[k // 2])
+        def wpe_mm(g, tag="ii"):
+            n = PE_UNITS[g]
+            if n:
+                wp = bank(tag, n * C, BF16)
                 for i in range(n):
-                    u = G_UNITS[g] + k + i
+                    u = G_UNITS[g] + i
                     nc.tensor.matmul(
                         wp[:, i * C:(i + 1) * C], lhsT=identb[:],
                         rhs=wraw[g][:].rearrange("p m w n -> p (m w) n")[:, u, :].rearrange("p (j f) -> p f j", j=4),
                         start=True, stop=True,
                     )
-                wps[g].append((G_UNITS[g] + k, n, wp))
+                wps[g] = wp
 
         def wpe_cp(g):
-            for u, n, wp in wps.get(g, []):
-                nc.scalar.copy(out=wgrp[g][:, u * C:(u + n) * C], in_=wp[:])
+            if g in wps:
+                u, n = G_UNITS[g], PE_UNITS[g]
+                nc.scalar.copy(out=wgrp[g][:, u * C:(u + n) * C], in_=wps[g][:])
 
-        def quant_x(g, h=None):
+        def quant_x(g, w0, w1):
             if g not in xcod:
                 xcod[g] = cd_pool.tile([P, 2 * WC * P], U32, name="xc", tag="xc", align_bytes=64)
                 xscl[g] = cd_pool.tile([P, 2 * WC * P], U8, name="xs", tag="xs", align_bytes=64)
-            lo, hi = (0, 2 * WC * P) if h is None else (h * WC * P, (h + 1) * WC * P)
+            lo, hi = 2 * w0 * P, 2 * w1 * P
             nc.vector.quantize_mx(out=xcod[g][:, lo:hi].bitcast(FP8X4), scales=xscl[g][:, lo:hi], in_=xgrp[g][:, 4 * lo:4 * hi])
 
         def quant_w(g):
@@ -206,175 +214,12 @@ def tile_dot_pa_kernel(tc, x_crop_bytes, x_crop_scale, W_r, W_i, b_r, b_i, out):
             nc.vector.quantize_mx(out=cod[:].bitcast(FP8X4), scales=scl[:], in_=wgrp[g][:])
             wcod[g], wscl[g] = cod, scl
 
-        def mm(g, ws=(0, 1, 2, 3)):
-            if g not in acc:
-                rr = acc_pool.tile([P, WC * P], F32, name="rr", tag="rr")
-                ii = acc_pool.tile([P, WC * P], F32, name="ii", tag="ii")
-                pi = acc_pool.tile([P, WC * P], F32, name="pi", tag="pi")
-                acc[g] = (rr, ii, pi)
-            rr, ii, pi = acc[g]
-
-            def mx(dst, w, m, c, start, stop):
-                ws_ = slice((m * WC + w) * F, (m * WC + w + 1) * F)
-                xs_ = slice((2 * w + c) * P, (2 * w + c + 1) * P)
-                nc.tensor.matmul_mx(
-                    out=dst[:, w * P:(w + 1) * P],
-                    lhsT=wcod[g][:, ws_].bitcast(FP8X4),
-                    lhsT_scale=wscl[g][:, ws_],
-                    rhs=xcod[g][:, xs_].bitcast(FP8X4),
-                    rhs_scale=xscl[g][:, xs_],
-                    start=start,
-                    stop=stop,
-                )
-
-            for w in ws:
-                mx(ii, w, 1, 1, True, True)
-            for w in ws:
-                mx(rr, w, 0, 0, True, True)
-            for w in ws:
-                mx(pi, w, 0, 1, True, False)
-                mx(pi, w, 1, 0, False, True)
-
-        def e1t(g):
-            t = ep_pool.tile([P, WC * P], F32, name="t", tag="t")
-            nc.scalar.activation(out=t[:], in_=acc[g][1][:], func=ACT.Identity, bias=brc[:], scale=-1.0)
-            tt[g] = t
-            if g not in V_SUM:
-                r = ep_pool.tile([P, WC * P], F32, name="r1", tag="r1")
-                nc.scalar.copy(out=r[:], in_=acc[g][0][:])
-                r1s[g] = r
-
-        def e1i(g):
-            i1 = ep_pool.tile([P, WC * P], F32, name="i1", tag="i1")
-            nc.scalar.activation(out=i1[:], in_=acc[g][2][:], func=ACT.Relu, bias=bic[:], scale=1.0)
-            i1s[g] = i1
-
-        def r1(g):
-            if g not in V_SUM:
-                return
-            r = ep_pool.tile([P, WC * P], F32, name="r1", tag="r1")
-            nc.vector.tensor_tensor(out=r[:], in0=acc[g][0][:], in1=tt[g][:], op=ALU.add)
-            r1s[g] = r
-
-        def tout(g, src, spare=False):
-            if spare:
-                to = tx_pool.tile([P, WC * F], F32, name="tx", tag="tx")
-            else:
-                to = acc_pool.tile([P, WC * F], F32, name="to", tag="to")
-            for w in range(WC):
-                if src is r1s and g not in V_SUM:
-                    nc.tensor.matmul(
-                        to[:, w * F:(w + 1) * F], lhsT=r1s[g][:, w * P:(w + 1) * P], rhs=ident[:],
-                        start=True, stop=False, is_transpose=True,
-                    )
-                    nc.tensor.matmul(
-                        to[:, w * F:(w + 1) * F], lhsT=tt[g][:, w * P:(w + 1) * P], rhs=ident[:],
-                        start=False, stop=True, is_transpose=True,
-                    )
-                else:
-                    nc.tensor.transpose(to[:, w * F:(w + 1) * F], src[g][:, w * P:(w + 1) * P], ident[:])
-            return to
-
-        def e2i(g):
-            ots[g] = ot_pool.tile([P, 2 * WC * F], F32, name="ot", tag="ot")
-            nc.scalar.copy(out=ots[g][:, WC * F:], in_=tos[g][:])
-
-        def e2r(g):
-            nc.scalar.activation(out=ots[g][:, 0:WC * F], in_=tos[g][:], func=ACT.Relu)
-            nc.sync.dma_start(
-                out=out[:, :, g, :, :].rearrange("b c w f -> b c (w f)"),
-                in_=ots[g][:].rearrange("p (c n) -> p c n", c=2),
-            )
-
-        hacc, ht, hr, hi1, hto = {}, {}, {}, {}, {}
-
-        def mm_half(g, h):
-            if h == 0:
-                rr = acc_pool.tile([P, 2 * P], F32, name="rr", tag="rr")
-                ii = acc_pool.tile([P, 2 * P], F32, name="ii", tag="ii")
-                pi = acc_pool.tile([P, 2 * P], F32, name="pi", tag="pi")
-            else:
-                ii = tx_pool.tile([P, 2 * P], F32, name="tx", tag="tx")
-                rr = tx_pool.tile([P, 2 * P], F32, name="tx", tag="tx")
-                pi = tx_pool.tile([P, 2 * P], F32, name="tx", tag="tx")
-            hacc[h] = (rr, ii, pi)
-
-            def mx(dst, w, m, c, start, stop):
-                ws_ = slice((m * WC + w) * F, (m * WC + w + 1) * F)
-                xs_ = slice((2 * w + c) * P, (2 * w + c + 1) * P)
-                nc.tensor.matmul_mx(
-                    out=dst[:, (w - 2 * h) * P:(w - 2 * h + 1) * P],
-                    lhsT=wcod[g][:, ws_].bitcast(FP8X4),
-                    lhsT_scale=wscl[g][:, ws_],
-                    rhs=xcod[g][:, xs_].bitcast(FP8X4),
-                    rhs_scale=xscl[g][:, xs_],
-                    start=start,
-                    stop=stop,
-                )
-
-            ws = (2 * h, 2 * h + 1)
-            for w in ws:
-                mx(ii, w, 1, 1, True, True)
-            for w in ws:
-                mx(rr, w, 0, 0, True, True)
-            for w in ws:
-                mx(pi, w, 0, 1, True, False)
-                mx(pi, w, 1, 0, False, True)
-
-        def e1_half(h, rr_on_vector):
-            rr, ii, pi = hacc[h]
-            ht[h] = ep_pool.tile([P, 2 * P], F32, name="t", tag="t")
-            hr[h] = ep_pool.tile([P, 2 * P], F32, name="r1", tag="r1")
-            hi1[h] = ep_pool.tile([P, 2 * P], F32, name="i1", tag="i1")
-            nc.scalar.activation(out=ht[h][:], in_=ii[:], func=ACT.Identity, bias=brc[:], scale=-1.0)
-            if rr_on_vector:
-                nc.vector.tensor_copy(out=hr[h][:], in_=rr[:])
-            else:
-                nc.scalar.copy(out=hr[h][:], in_=rr[:])
-            nc.scalar.activation(out=hi1[h][:], in_=pi[:], func=ACT.Relu, bias=bic[:], scale=1.0)
-
-        def tout_half(h, spare):
-            if spare:
-                to = tx_pool.tile([P, 4 * F], F32, name="tx", tag="tx")
-            else:
-                to = acc_pool.tile([P, 4 * F], F32, name="to", tag="to")
-            for w in range(2):
-                nc.tensor.matmul(to[:, w * F:(w + 1) * F], lhsT=hr[h][:, w * P:(w + 1) * P], rhs=ident[:], start=True, stop=False, is_transpose=True)
-                nc.tensor.matmul(to[:, w * F:(w + 1) * F], lhsT=ht[h][:, w * P:(w + 1) * P], rhs=ident[:], start=False, stop=True, is_transpose=True)
-            for w in range(2):
-                nc.tensor.transpose(to[:, (2 + w) * F:(3 + w) * F], hi1[h][:, w * P:(w + 1) * P], ident[:])
-            hto[h] = to
-
-        def e2_half(g, h, queue):
-            o = ot_pool.tile([P, 4 * F], F32, name="ot", tag="ot")
-            nc.scalar.activation(out=o[:], in_=hto[h][:], func=ACT.Relu)
-            queue.dma_start(
-                out=out[:, :, g, 2 * h:2 * h + 2, :].rearrange("b c w f -> b c (w f)"),
-                in_=o[:].rearrange("p (c n) -> p c n", c=2),
-            )
-
-        pacc, pt, pr, pi1, pto = {}, {}, {}, {}, {}
-
-        def quant_x_px(g, w0, w1):
-            if g not in xcod:
-                xcod[g] = cd_pool.tile([P, 2 * WC * P], U32, name="xc", tag="xc", align_bytes=64)
-                xscl[g] = cd_pool.tile([P, 2 * WC * P], U8, name="xs", tag="xs", align_bytes=64)
-            lo, hi = 2 * w0 * P, 2 * w1 * P
-            nc.vector.quantize_mx(out=xcod[g][:, lo:hi].bitcast(FP8X4), scales=xscl[g][:, lo:hi], in_=xgrp[g][:, 4 * lo:4 * hi])
-
-        def mm_piece(g, ws, one_bank):
+        def mm(g, ws=(0, 1, 2, 3), tags=("rr", "ii", "pi")):
             n = len(ws)
-            if one_bank:
-                iit = tx_pool.tile([P, n * P], F32, name="tx", tag="tx")
-                rrt = tx_pool.tile([P, n * P], F32, name="tx", tag="tx")
-                pit = tx_pool.tile([P, n * P], F32, name="tx", tag="tx")
-                ii, rr, pi = iit[:], rrt[:], pit[:]
-            else:
-                rrt = acc_pool.tile([P, n * P], F32, name="rr", tag="rr")
-                iit = acc_pool.tile([P, n * P], F32, name="ii", tag="ii")
-                pit = acc_pool.tile([P, n * P], F32, name="pi", tag="pi")
-                ii, rr, pi = iit[:], rrt[:], pit[:]
-            pacc[ws] = (rr, ii, pi)
+            rr = bank(tags[0], n * P)
+            ii = bank(tags[1], n * P)
+            pi = bank(tags[2], n * P)
+            acc[g, ws] = (rr, ii, pi)
 
             def mx(dst, w, m, c, start, stop):
                 ws_ = slice((m * WC + w) * F, (m * WC + w + 1) * F)
@@ -397,40 +242,80 @@ def tile_dot_pa_kernel(tc, x_crop_bytes, x_crop_scale, W_r, W_i, b_r, b_i, out):
                 mx(pi, w, 0, 1, True, False)
                 mx(pi, w, 1, 0, False, True)
 
-        def e1_piece(ws, rr_on_vector):
-            n = len(ws)
-            rr, ii, pi = pacc[ws]
-            pt[ws] = ep_pool.tile([P, n * P], F32, name="t", tag="t")
-            pr[ws] = ep_pool.tile([P, n * P], F32, name="r1", tag="r1")
-            pi1[ws] = ep_pool.tile([P, n * P], F32, name="i1", tag="i1")
-            nc.scalar.activation(out=pt[ws][:], in_=ii, func=ACT.Identity, bias=brc[:], scale=-1.0)
-            if rr_on_vector:
-                nc.vector.tensor_copy(out=pr[ws][:], in_=rr)
-            else:
-                nc.scalar.copy(out=pr[ws][:], in_=rr)
-            nc.scalar.activation(out=pi1[ws][:], in_=pi, func=ACT.Relu, bias=bic[:], scale=1.0)
+        ALLW = (0, 1, 2, 3)
 
-        def tout_piece(ws, spare):
-            n = len(ws)
-            if spare:
-                to = tx_pool.tile([P, 2 * n * F], F32, name="tx", tag="tx")
+        def e1_t(g, ws=ALLW):
+            t = ep_pool.tile([P, len(ws) * P], F32, name="t", tag="t")
+            nc.scalar.activation(out=t[:], in_=acc[g, ws][1][:], func=ACT.Identity, bias=brc[:], scale=-1.0)
+            tt[g, ws] = t
+
+        def e1_r(g, ws=ALLW, on_vector=False):
+            r = ep_pool.tile([P, len(ws) * P], F32, name="r1", tag="r1")
+            if on_vector:
+                nc.vector.tensor_copy(out=r[:], in_=acc[g, ws][0][:])
             else:
-                to = acc_pool.tile([P, 2 * n * F], F32, name="to", tag="to")
-            for w in range(n):
-                nc.tensor.matmul(to[:, w * F:(w + 1) * F], lhsT=pr[ws][:, w * P:(w + 1) * P], rhs=ident[:], start=True, stop=False, is_transpose=True)
-                nc.tensor.matmul(to[:, w * F:(w + 1) * F], lhsT=pt[ws][:, w * P:(w + 1) * P], rhs=ident[:], start=False, stop=True, is_transpose=True)
-            for w in range(n):
-                nc.tensor.transpose(to[:, (n + w) * F:(n + w + 1) * F], pi1[ws][:, w * P:(w + 1) * P], ident[:])
+                nc.scalar.copy(out=r[:], in_=acc[g, ws][0][:])
+            r1s[g, ws] = r
+
+        def e1_i(g, ws=ALLW, on_vector=False):
+            i1 = ep_pool.tile([P, len(ws) * P], F32, name="i1", tag="i1")
+            if on_vector:
+                nc.vector.tensor_scalar(out=i1[:], in0=acc[g, ws][2][:], scalar1=bic[:], scalar2=0.0, op0=ALU.add, op1=ALU.max)
+            else:
+                nc.scalar.activation(out=i1[:], in_=acc[g, ws][2][:], func=ACT.Relu, bias=bic[:], scale=1.0)
+            i1s[g, ws] = i1
+
+        def back_r(to, col, g, ws):
+            for k in range(len(ws)):
+                dst = to[:, (col + k) * F:(col + k + 1) * F]
+                nc.tensor.matmul(dst, lhsT=r1s[g, ws][:, k * P:(k + 1) * P], rhs=ident[:], start=True, stop=False, is_transpose=True)
+                nc.tensor.matmul(dst, lhsT=tt[g, ws][:, k * P:(k + 1) * P], rhs=ident[:], start=False, stop=True, is_transpose=True)
+
+        def back_i(to, col, g, ws):
+            for k in range(len(ws)):
+                nc.tensor.transpose(to[:, (col + k) * F:(col + k + 1) * F], i1s[g, ws][:, k * P:(k + 1) * P], ident[:])
+
+        def tout_r(g, tag="to"):
+            tos[g] = bank(tag, WC * F)
+            back_r(tos[g], 0, g, ALLW)
+
+        def tout_i(g, tag="to"):
+            tos[g] = bank(tag, WC * F)
+            back_i(tos[g], 0, g, ALLW)
+
+        def e2i(g):
+            if g not in ots:
+                ots[g] = ot_pool.tile([P, 2 * WC * F], F32, name="ot", tag="ot")
+            nc.scalar.copy(out=ots[g][:, WC * F:], in_=tos[g][:])
+
+        def e2r(g):
+            if g not in ots:
+                ots[g] = ot_pool.tile([P, 2 * WC * F], F32, name="ot", tag="ot")
+            nc.scalar.activation(out=ots[g][:, 0:WC * F], in_=tos[g][:], func=ACT.Relu)
+
+        def store(g):
+            nc.sync.dma_start(
+                out=out[:, :, g, :, :].rearrange("b c w f -> b c (w f)"),
+                in_=ots[g][:].rearrange("p (c n) -> p c n", c=2),
+            )
+
+        pto = {}
+
+        def tout_piece(g, ws, tag):
+            n = len(ws)
+            to = bank(tag, 2 * n * F)
+            back_r(to, 0, g, ws)
+            back_i(to, n, g, ws)
             pto[ws] = to
 
-        def e2_piece(g, ws, queue, on_vector=False):
+        def e2_piece(g, ws, on_vector=False):
             n = len(ws)
             o = ot_pool.tile([P, 2 * n * F], F32, name="ot", tag="ot")
             if on_vector:
                 nc.vector.tensor_scalar_max(out=o[:], in0=pto[ws][:], scalar1=0.0)
             else:
                 nc.scalar.activation(out=o[:], in_=pto[ws][:], func=ACT.Relu)
-            queue.dma_start(
+            nc.sync.dma_start(
                 out=out[:, :, g, ws[0]:ws[0] + n, :].rearrange("b c w f -> b c (w f)"),
                 in_=o[:].rearrange("p (c n) -> p c n", c=2),
             )
@@ -438,319 +323,140 @@ def tile_dot_pa_kernel(tc, x_crop_bytes, x_crop_scale, W_r, W_i, b_r, b_i, out):
         def quants(g):
             if QW_FIRST:
                 quant_w(g)
-                quant_x(g)
-            elif QX_SPLIT == 2:
-                quant_x(g, 0)
-                quant_w(g)
-                quant_x(g, 1)
-            elif QX_SPLIT:
-                quant_x(g, 0)
-                quant_x(g, 1)
-                quant_w(g)
+                quant_x(g, 0, 4)
             else:
-                quant_x(g)
+                quant_x(g, 0, 2)
                 quant_w(g)
+                quant_x(g, 2, 4)
 
-        if HEAD == 1:
-            load_x_px(0, 0, 1)
-            load_x_px(0, 1, 2)
-            load_w(0, 0)
-            load_x_px(0, 2, WC)
-            load_w(0, 1)
-        elif HEAD == 2:
-            load_x_px(0, 0, 1)
-            load_x_px(0, 1, 2)
-            load_x_px(0, 2, WC)
-            load_w(0, 0)
-            load_w(0, 1)
-        elif HEAD == 3:
-            load_x_px(0, 0, 1)
-            load_w(0, 0)
-            load_x_px(0, 1, WC)
-            load_w(0, 1)
-        elif FINE0 == 1:
-            load_x_px(0, 0, 2)
-            load_w_px(0, 0, 0, 2)
-            load_x_px(0, 2, WC)
-            load_w_px(0, 0, 2, 4)
-            load_w(0, 1)
-        elif FINE0 == 5:
-            load_x_px(0, 0, 1)
-            load_x_px(0, 1, 2)
-            load_w_px(0, 0, 0, 2)
-            load_x_px(0, 2, WC)
-            load_w_px(0, 0, 2, 4)
-            load_w(0, 1)
-        elif FINE0 == 6:
-            load_x_px(0, 0, 1)
-            load_w_px(0, 0, 0, 2)
-            load_x_px(0, 1, 2)
-            load_x_px(0, 2, WC)
-            load_w_px(0, 0, 2, 4)
-            load_w(0, 1)
-        elif FINE0 == 4:
-            load_x_px(0, 0, 2)
-            load_x_px(0, 2, WC)
-            load_w_px(0, 0, 0, 2)
-            load_x_px(1, 0, 2)
-            load_w_px(0, 0, 2, 4)
-            load_x_px(1, 2, WC)
-            load_w(0, 1)
-        elif FINE0 == 3:
-            load_x_px(0, 0, 2)
-            load_x_px(0, 2, WC)
-            load_w_px(0, 0, 0, 2)
-            load_w_px(0, 0, 2, 4)
-            load_w(0, 1)
-        elif FINE0 == 2:
-            load_x_px(0, 0, 2)
-            load_w_px(0, 0, 0, 2)
-            load_x_px(0, 2, WC)
-            load_w_px(0, 0, 2, 4)
-            load_w_px(0, 1, 0, 2)
-            load_w_px(0, 1, 2, 4)
-        else:
-            load_x_px(0, 0, 2)
-            load_w(0, 0)
-            load_x_px(0, 2, WC)
-            load_w(0, 1)
-        if FINE0 != 4:
-            load_x_px(1, 0, WC)
+        load_x(0, 0, 1)
+        load_x(0, 1, 2)
+        load_w(0, 0, 0, 2)
+        load_x(0, 2, WC)
+        load_w(0, 0, 2, 4)
+        load_w(0, 1)
+        load_x(1, 0, WC)
         for g in range(2, HC):
-            if not WX_ORDER:
-                load_x_px(g, 0, WC)
             load_w(g - 1, 0)
             load_w(g - 1, 1)
-            if WX_ORDER:
-                load_x_px(g, 0, WC)
+            load_x(g, 0, WC)
         load_w(HC - 1, 0)
         load_w(HC - 1, 1)
 
-        def has(g):
-            return 0 <= g < HC
-
-        if HEAD:
-            for w in range(WC):
-                cast_px(0, w, w + 1, on_vector=(w == 0))
-            txp(0)
-            wil_g(0, (0, WC, G_UNITS[0]))
-            wpe_mm(0)
-            wil_s(0)
-            wpe_cp(0)
-            cast_px(1, 0, 2)
-            cast_px(1, 2, 4)
+        if NEW_HEAD >= 1:
+            cast(0, 0, C, on_vector=True)
+            cast(0, GW, GW + C)
         else:
-            if FINE0 in (5, 6):
-                cast_px(0, 0, 1, on_vector=True)
-                cast_px(0, 1, 2)
-                cast_px(0, 2, 4)
-            else:
-                cast_px(0, 0, 2, on_vector=(VHEAD >= 0))
-                cast(0, 2 * C, 4 * C, VHEAD >= 1)
-                cast(0, GW + 2 * C, GW + 4 * C, VHEAD >= 2)
-            if FINE0 in (1, 3, 4, 5, 6):
-                wil_g(0, (0, 2, WC, G_UNITS[0]))
-            elif FINE0 == 2:
-                wil_g(0, (0, 2, WC, 6, G_UNITS[0]))
-            elif G_UNITS[0] > WC:
-                wil_g(0, (0, WC, G_UNITS[0]))
-            else:
-                wil_g(0)
-            if PE0_AT == 0:
-                txp(0)
-                wpe_mm(0)
-            elif PE0_AT == 1:
-                txp(0, (0, 1))
-                wpe_mm(0)
-                txp(0, (2, 3))
-            else:
-                txp(0, (0, 1, 2))
-                wpe_mm(0)
-                txp(0, (3,))
-            wpe_cp(0)
-            if WS0_EARLY == 1:
-                wil_s(0)
-            cast_px(1, 0, 2)
-            if WS0_EARLY == 2:
-                wil_s(0)
-            cast_px(1, 2, 4)
-            if not WS0_EARLY:
-                wil_s(0)
+            cast_px(0, 0, 1, on_vector=True)
+        cast_px(0, 1, 2)
+        if NEW_HEAD >= 2:
+            cast_px(0, 2, 3)
+            cast_px(0, 3, 4)
+        else:
+            cast_px(0, 2, 4)
+        wil_g(0, (0, 2, WC, G_UNITS[0]))
+        txp(0)
+        wil_s(0)
+        cast_px(1, 0, 2)
+        cast_px(1, 2, 4)
         nc.scalar.copy(out=brc[:], in_=brb[:])
         nc.scalar.copy(out=bic[:], in_=bib[:])
         em(0)
         txp(1)
         last = HC - 1
-        st2 = {"cur": -1, "next": 0}
         for j in range(last):
-            if VCAST and has(j + 2):
-                cast(j + 2, 2 * GW - VCAST, 2 * GW, on_vector=True)
+            more = j + 2 < HC
             quants(j)
-            if has(j - 1):
-                r1(j - 1)
-            if SHAKE:
-                new_xg(j + 1)
             wil_g(j + 1)
-            if has(j + 2):
+            if j in WS_FIRST:
+                wil_s(j + 1)
+            if P_AT == 0:
+                em_p_planes(j + 1)
+            if more:
                 cast(j + 2, 0, GW)
-            wil_s(j + 1)
-            ge = st2["cur"] if E2N[j] else -1
-            if ge >= 0:
-                e2i(ge)
+            if P_AT == 1:
+                em_p_planes(j + 1)
+            if j not in WS_FIRST:
+                wil_s(j + 1)
+            if j >= 1:
+                e2i(j - 1)
             mm(j)
-            if ge >= 0:
-                tos[ge] = tout(ge, r1s)
-            if S0_AHEAD and j == 0:
-                wpe_mm(1, ("to",))
-                cast(2, GW, GW + GW // 2)
-                wpe_cp(1)
-                cast(2, GW + GW // 2, 2 * GW - VCAST)
-                e1t(0)
-                e1i(0)
-            else:
-                e1t(j)
-                wpe_mm(j + 1)
-            if S0_AHEAD and j == 0:
-                pass
-            elif CPW_MID:
-                if has(j + 2):
-                    cast(j + 2, GW, GW + GW // 2)
-                wpe_cp(j + 1)
-                if has(j + 2):
-                    cast(j + 2, GW + GW // 2, 2 * GW - VCAST)
-                e1i(j)
-            else:
-                if has(j + 2):
-                    cast(j + 2, GW, 2 * GW - VCAST)
-                e1i(j)
-                wpe_cp(j + 1)
-            if ge >= 0:
-                e2r(ge)
-                st2["cur"] = -1
-                st2["next"] = ge + 1
-            for extra in range(E2N[j] - 1):
-                gx = st2["next"]
-                tos[gx] = tout(gx, i1s)
-                e2i(gx)
-                tos[gx] = tout(gx, r1s)
-                e2r(gx)
-                st2["next"] = gx + 1
-            if TAIL == 3 and j == last - 1:
-                em(last, (0, 1, 2))
-                quant_w(last)
-                quant_x_px(last, 0, 2)
-                quant_x_px(last, 2, 3)
-                em(last, (3,))
-                quant_x_px(last, 3, 4)
-            elif TAIL and j == last - 1:
-                em(last, (0, 1, 2))
-                quant_w(last)
-                quant_x(last, 0)
-                em(last, (3,))
-                if TAIL == 2:
-                    quant_x(last, 1)
-            else:
+            if j >= 1:
+                tout_r(j - 1)
+            e1_t(j)
+            e1_r(j)
+            wpe_mm(j + 1)
+            em_p_mm(j + 1)
+            if more:
+                cast(j + 2, GW, GW + GW // 2)
+            wpe_cp(j + 1)
+            new_xg(j + 1)
+            em_p_cp(j + 1)
+            if more:
+                cast(j + 2, GW + GW // 2, 2 * GW)
+            e1_i(j)
+            if j >= 1:
+                e2r(j - 1)
+                store(j - 1)
+            if j < last - 1:
                 em(j + 1)
-            if has(j + 2):
-                txp(j + 2)
-            if st2["cur"] < 0:
-                gn = st2["next"]
-                tos[gn] = tout(gn, i1s)
-                st2["cur"] = gn
-
-        if TAIL == 3:
-            pa, pb, pc = (0, 1), (2,), (3,)
-            r1(last - 1)
-            e2i(last - 1)
-        if TAIL == 3 and T3_ORDER == 2:
-            mm_piece(last, pa, False)
-            mm_piece(last, pb, True)
-            tos[last - 1] = tout(last - 1, r1s)
-            e1_piece(pa, False)
-            e2r(last - 1)
-            e1_piece(pb, False)
-            mm_piece(last, pc, False)
-            tout_piece(pa, True)
-            e1_piece(pc, True)
-            tout_piece(pb, False)
-            tout_piece(pc, True)
-            e2_piece(last, pa, nc.sync, True)
-            e2_piece(last, pb, nc.sync, True)
-            e2_piece(last, pc, nc.sync)
-        elif TAIL == 3 and T3_ORDER == 3:
-            mm_piece(last, pa, False)
-            mm_piece(last, pb, True)
-            e1_piece(pa, False)
-            tos[last - 1] = tout(last - 1, r1s)
-            e1_piece(pb, False)
-            mm_piece(last, pc, False)
-            e2r(last - 1)
-            tout_piece(pa, True)
-            e1_piece(pc, True)
-            tout_piece(pb, False)
-            tout_piece(pc, True)
-            e2_piece(last, pa, nc.sync, True)
-            e2_piece(last, pb, nc.sync, True)
-            e2_piece(last, pc, nc.sync)
-        elif TAIL == 3:
-            mm_piece(last, pa, False)
-            tos[last - 1] = tout(last - 1, r1s)
-            e1_piece(pa, False)
-            mm_piece(last, pb, True)
-            e2r(last - 1)
-            if T3_ORDER == 0:
-                tout_piece(pa, True)
-                e1_piece(pb, False)
-                mm_piece(last, pc, False)
-                e2_piece(last, pa, nc.sync, E2V >= 1)
-                tout_piece(pb, False)
-                e1_piece(pc, E2V < 2)
-                e2_piece(last, pb, nc.sync, E2V >= 2)
             else:
-                e1_piece(pb, False)
-                mm_piece(last, pc, False)
-                tout_piece(pa, True)
-                tout_piece(pb, False)
-                e1_piece(pc, True)
-                e2_piece(last, pa, nc.sync)
-                e2_piece(last, pb, nc.sync)
-            tout_piece(pc, True)
-            e2_piece(last, pc, nc.sync)
-        elif TAIL == 2:
-            r1(last - 1)
-            e2i(last - 1)
-            mm_half(last, 0)
-            tos[last - 1] = tout(last - 1, r1s)
-            e1_half(0, False)
+                em(last, (0, 1, 2))
+                quant_w(last)
+                quant_x(last, 0, 2)
+                quant_x(last, 2, 3)
+                em(last, (3,))
+                quant_x(last, 3, 4)
+            if more:
+                txp(j + 2)
+            if not (NEW_TAIL and j == last - 1):
+                tout_i(j)
+
+        pa, pb, pc = (0, 1), (2,), (3,)
+        if NEW_TAIL:
+            tout_r(last - 1, "tx0")
             e2r(last - 1)
-            tout_half(0, True)
-            mm_half(last, 1)
-            e2_half(last, 0, nc.sync)
-            e1_half(1, True)
-            tout_half(1, False)
-            e2_half(last, 1, nc.sync)
-        elif TAIL:
-            r1(last - 1)
-            quant_x(last, 1)
+            tout_i(last - 1, "tx1")
             e2i(last - 1)
-            mm(last, (0, 1))
-            tos[last - 1] = tout(last - 1, r1s)
-            mm(last, (2, 3))
-        else:
-            quants(last)
-            r1(last - 1)
-            e2i(last - 1)
-            tos[last - 1] = tout(last - 1, r1s)
-            mm(last)
-        if TAIL < 2:
-            e1t(last)
-            e2r(last - 1)
-            e1i(last)
-            r1(last)
-            tr_last = tout(last, r1s, spare=True)
-            ti_last = tout(last, i1s, spare=True)
-            ot = ot_pool.tile([P, 2 * WC * F], F32, name="ot", tag="ot")
-            nc.scalar.activation(out=ot[:, 0:WC * F], in_=tr_last[:], func=ACT.Relu)
-            nc.sync.dma_start(out=out[:, 0, last, :, :].rearrange("b w f -> b (w f)"), in_=ot[:, 0:WC * F])
-            nc.vector.tensor_copy(out=ot[:, WC * F:], in_=ti_last[:])
-            nc.scalar.dma_start(out=out[:, 1, last, :, :].rearrange("b w f -> b (w f)"), in_=ot[:, WC * F:])
+            store(last - 1)
+            mm(last, pa)
+            e1_t(last, pa)
+            e1_r(last, pa)
+            e1_i(last, pa)
+            mm(last, pb, ("tx2", "to", "tx0"))
+            tout_piece(last, pa, "tx1")
+            e1_t(last, pb)
+            e1_r(last, pb, on_vector=TV >= 2)
+            e1_i(last, pb)
+            mm(last, pc)
+            e2_piece(last, pa, on_vector=TV >= 1)
+            tout_piece(last, pb, "tx3")
+            e1_t(last, pc)
+            e1_r(last, pc, on_vector=True)
+            e1_i(last, pc, on_vector=TV >= 3)
+            e2_piece(last, pb, on_vector=TV >= 1)
+            tout_piece(last, pc, "tx2")
+            e2_piece(last, pc)
+            return
+        e2i(last - 1)
+        mm(last, pa)
+        tout_r(last - 1)
+        e1_t(last, pa)
+        e1_r(last, pa)
+        e1_i(last, pa)
+        mm(last, pb, ("tx1", "tx0", "tx2"))
+        e2r(last - 1)
+        store(last - 1)
+        tout_piece(last, pa, "tx3")
+        e1_t(last, pb)
+        e1_r(last, pb)
+        e1_i(last, pb)
+        mm(last, pc)
+        e2_piece(last, pa)
+        tout_piece(last, pb, "to")
+        e1_t(last, pc)
+        e1_r(last, pc, on_vector=True)
+        e1_i(last, pc)
+        e2_piece(last, pb)
+        tout_piece(last, pc, "tx0")
+        e2_piece(last, pc)

@@ -25,6 +25,9 @@ TV = 1
 WS_FIRST = ()
 P_EM = {}
 P_AT = 0
+TQ = 1
+RPC_V = 1
+LASTX = 1
 NEW_HEAD = 0
 WARM_PE = 0
 LATE_BIAS = 0
@@ -67,6 +70,12 @@ def tile_dot_pa_kernel(tc, x_crop_bytes, x_crop_scale, W_r, W_i, b_r, b_i, out):
 
         if not LATE_BIAS:
             load_bias()
+        if WARM_PE:
+            wz = const.tile([P, C], BF16, name="wz", tag="wz")
+            nc.vector.memset(wz[:], 0.0)
+            dummy = bank("to", C)
+            for k in range(WARM_PE):
+                nc.tensor.matmul(dummy[:], lhsT=wz[:, 0:P], rhs=wz[:], start=True, stop=True)
         ident = const.tile([P, P], F32, name="ident", tag="ident")
         make_identity(nc, ident[:])
         identb = const.tile([P, P], BF16, name="identb", tag="identb")
@@ -320,6 +329,46 @@ def tile_dot_pa_kernel(tc, x_crop_bytes, x_crop_scale, W_r, W_i, b_r, b_i, out):
                 in_=o[:].rearrange("p (c n) -> p c n", c=2),
             )
 
+        def last_pixel(g, w):
+            za = bank("rr", 2 * F)
+            zb = bank("ii", F)
+
+            def mx(dst, m, c, start, stop):
+                ws_ = slice((m * WC + w) * F, (m * WC + w + 1) * F)
+                xs_ = slice((2 * w + c) * P, (2 * w + c + 1) * P)
+                nc.tensor.matmul_mx(
+                    out=dst,
+                    lhsT=xcod[g][:, xs_].bitcast(FP8X4),
+                    lhsT_scale=xscl[g][:, xs_],
+                    rhs=wcod[g][:, ws_].bitcast(FP8X4),
+                    rhs_scale=wscl[g][:, ws_],
+                    start=start,
+                    stop=stop,
+                )
+
+            mx(zb[:], 1, 1, True, True)
+            mx(za[:, 0:F], 0, 0, True, True)
+            mx(za[:, F:2 * F], 0, 1, True, False)
+            mx(za[:, F:2 * F], 1, 0, False, True)
+            t = ep_pool.tile([P, F], F32, name="t", tag="t")
+            z = ep_pool.tile([P, 2 * F], F32, name="r1", tag="r1")
+            o = ot_pool.tile([P, 2 * F], F32, name="ot", tag="ot")
+            nc.vector.tensor_tensor(out=t[:], in0=bb[:, 0:F], in1=zb[:], op=ALU.subtract)
+            nc.vector.tensor_tensor(out=z[:, F:2 * F], in0=za[:, F:2 * F], in1=bb[:, F:2 * F], op=ALU.add)
+            nc.vector.tensor_tensor(out=z[:, 0:F], in0=za[:, 0:F], in1=t[:], op=ALU.add)
+            if LASTX == 2:
+                nc.scalar.activation(out=o[:, F:2 * F], in_=z[:, F:2 * F], func=ACT.Relu)
+                nc.vector.tensor_scalar_max(out=o[:, 0:F], in0=z[:, 0:F], scalar1=0.0)
+            else:
+                nc.vector.tensor_scalar_max(out=o[:], in0=z[:], scalar1=0.0)
+            return o
+
+        def last_store(g, w, o):
+            nc.sync.dma_start(
+                out=out[:, :, g, w:w + 1, :].rearrange("b c w f -> b c (w f)"),
+                in_=o[:].rearrange("p (c n) -> p c n", c=2),
+            )
+
         def quants(g):
             if QW_FIRST:
                 quant_w(g)
@@ -342,6 +391,10 @@ def tile_dot_pa_kernel(tc, x_crop_bytes, x_crop_scale, W_r, W_i, b_r, b_i, out):
             load_x(g, 0, WC)
         load_w(HC - 1, 0)
         load_w(HC - 1, 1)
+        if LASTX:
+            bb = const.tile([P, 2 * F], BF16, name="bb", tag="bb")
+            nc.sync.dma_start(out=bb[:, 0:F], in_=b_r.partition_broadcast(P))
+            nc.sync.dma_start(out=bb[:, F:2 * F], in_=b_i.partition_broadcast(P))
 
         if NEW_HEAD >= 1:
             cast(0, 0, C, on_vector=True)
@@ -354,6 +407,8 @@ def tile_dot_pa_kernel(tc, x_crop_bytes, x_crop_scale, W_r, W_i, b_r, b_i, out):
             cast_px(0, 3, 4)
         else:
             cast_px(0, 2, 4)
+        if LATE_BIAS:
+            load_bias()
         wil_g(0, (0, 2, WC, G_UNITS[0]))
         txp(0)
         wil_s(0)
@@ -402,8 +457,12 @@ def tile_dot_pa_kernel(tc, x_crop_bytes, x_crop_scale, W_r, W_i, b_r, b_i, out):
                 em(j + 1)
             else:
                 em(last, (0, 1, 2))
-                quant_w(last)
-                quant_x(last, 0, 2)
+                if TQ:
+                    quant_x(last, 0, 2)
+                    quant_w(last)
+                else:
+                    quant_w(last)
+                    quant_x(last, 0, 2)
                 quant_x(last, 2, 3)
                 em(last, (3,))
                 quant_x(last, 3, 4)
@@ -428,11 +487,18 @@ def tile_dot_pa_kernel(tc, x_crop_bytes, x_crop_scale, W_r, W_i, b_r, b_i, out):
             e1_t(last, pb)
             e1_r(last, pb, on_vector=TV >= 2)
             e1_i(last, pb)
+            if LASTX:
+                o3 = last_pixel(last, 3)
+                e2_piece(last, pa)
+                tout_piece(last, pb, "tx3")
+                e2_piece(last, pb)
+                last_store(last, 3, o3)
+                return
             mm(last, pc)
             e2_piece(last, pa, on_vector=TV >= 1)
             tout_piece(last, pb, "tx3")
             e1_t(last, pc)
-            e1_r(last, pc, on_vector=True)
+            e1_r(last, pc, on_vector=RPC_V)
             e1_i(last, pc, on_vector=TV >= 3)
             e2_piece(last, pb, on_vector=TV >= 1)
             tout_piece(last, pc, "tx2")

@@ -28,8 +28,8 @@ P_AT = 0
 TQ = 1
 RPC_V = 1
 LASTX = 1
-NEW_HEAD = 0
-WARM_PE = 0
+NEW_HEAD = 2
+WARM_PE = 6
 LATE_BIAS = 0
 
 

@@ -22,12 +22,12 @@ PE_UNITS = (0, 1, 1, 1, 1, 1, 1, 0)
 QW_FIRST = 0
 NEW_TAIL = 1
 TV = 1
-WS_FIRST = ()
+WS_FIRST = (0,)
 P_EM = {}
 P_AT = 0
 TQ = 1
 RPC_V = 1
-LASTX = 1
+LASTX = 3
 NEW_HEAD = 2
 WARM_PE = 6
 LATE_BIAS = 0
@@ -329,9 +329,9 @@ def tile_dot_pa_kernel(tc, x_crop_bytes, x_crop_scale, W_r, W_i, b_r, b_i, out):
                 in_=o[:].rearrange("p (c n) -> p c n", c=2),
             )
 
-        def last_pixel(g, w):
-            za = bank("rr", 2 * F)
-            zb = bank("ii", F)
+        def last_pixel(g, w, tags=("rr", "ii")):
+            za = bank(tags[0], 2 * F)
+            zb = bank(tags[1], F)
 
             def mx(dst, m, c, start, stop):
                 ws_ = slice((m * WC + w) * F, (m * WC + w + 1) * F)
@@ -456,8 +456,16 @@ def tile_dot_pa_kernel(tc, x_crop_bytes, x_crop_scale, W_r, W_i, b_r, b_i, out):
             if j < last - 1:
                 em(j + 1)
             else:
-                em(last, (0, 1, 2))
-                if TQ:
+                if TQ == 2:
+                    em(last, (0, 1))
+                    quant_x(last, 0, 2)
+                    quant_w(last)
+                    em(last, (2,))
+                else:
+                    em(last, (0, 1, 2))
+                if TQ == 2:
+                    pass
+                elif TQ:
                     quant_x(last, 0, 2)
                     quant_w(last)
                 else:
@@ -482,6 +490,14 @@ def tile_dot_pa_kernel(tc, x_crop_bytes, x_crop_scale, W_r, W_i, b_r, b_i, out):
             e1_t(last, pa)
             e1_r(last, pa)
             e1_i(last, pa)
+            if LASTX == 3:
+                o2 = last_pixel(last, 2, ("tx2", "to"))
+                tout_piece(last, pa, "tx1")
+                o3 = last_pixel(last, 3)
+                last_store(last, 2, o2)
+                e2_piece(last, pa)
+                last_store(last, 3, o3)
+                return
             mm(last, pb, ("tx2", "to", "tx0"))
             tout_piece(last, pa, "tx1")
             e1_t(last, pb)

@@ -141,8 +141,8 @@ def tile_dot_pa_kernel(tc, x_crop_bytes, x_crop_scale, W_r, W_i, b_r, b_i, out):
                     continue
                 nc.vector.tensor_tensor(
                     out=xg[:, w * 2 * C:(w + 1) * 2 * C].rearrange("p (n u e) -> p n u e", u=2, e=2),
-                    in0=txs[g, w][:].bitcast(BF16).rearrange("p (u n e) -> p n u e", u=2, e=2),
-                    in1=sct[:].to_broadcast([P, 2 * P, 2, 2]),
+                    in0=sct[:].to_broadcast([P, 2 * P, 2, 2]),
+                    in1=txs[g, w][:].bitcast(BF16).rearrange("p (u n e) -> p n u e", u=2, e=2),
                     op=ALU.mult,
                 )
 

from contextlib import ExitStack

import concourse.mybir as mybir
from concourse.masks import make_identity

F32 = mybir.dt.float32
BF16 = mybir.dt.bfloat16
U32 = mybir.dt.uint32
U8 = mybir.dt.uint8
FP8 = mybir.dt.float8_e4m3fn
FP8X4 = mybir.dt.float8_e4m3fn_x4
ALU = mybir.AluOpType
ACT = mybir.ActivationFunctionType

B, HC, WC, C, F = 128, 8, 4, 512, 128
P = 128
GW = WC * C
FLOPS = 4 * 2 * B * HC * WC * C * F

G_UNITS = (6, 6, 6, 6, 6, 6, 6, 5)
PE_UNITS = (0, 1, 1, 1, 1, 1, 1, 0)
QW_FIRST = 0
NEW_TAIL = 1
TV = 1
WS_FIRST = (0,)
P_EM = {}
P_AT = 0
TQ = 1
RPC_V = 1
LASTX = 3
NEW_HEAD = 2
WARM_PE = 6
LATE_BIAS = 0


def tile_dot_pa_kernel(tc, x_crop_bytes, x_crop_scale, W_r, W_i, b_r, b_i, out):
    nc = tc.nc
    with ExitStack() as ctx:
        const = ctx.enter_context(tc.tile_pool(name="const", bufs=1))
        xb_pool = ctx.enter_context(tc.tile_pool(name="xb_pool", bufs=HC))
        wr_pool = ctx.enter_context(tc.tile_pool(name="wr_pool", bufs=HC))
        xw_pool = ctx.enter_context(tc.tile_pool(name="xw_pool", bufs=3))
        xg_pool = ctx.enter_context(tc.tile_pool(name="xg_pool", bufs=2))
        wg_pool = ctx.enter_context(tc.tile_pool(name="wg_pool", bufs=1))
        cd_pool = ctx.enter_context(tc.tile_pool(name="cd_pool", bufs=2))
        ep_pool = ctx.enter_context(tc.tile_pool(name="ep_pool", bufs=2))
        ot_pool = ctx.enter_context(tc.tile_pool(name="ot_pool", bufs=5))
        pl_pool = ctx.enter_context(tc.tile_pool(name="pl_pool", bufs=1))
        ps_pool = ctx.enter_context(tc.psum_pool(name="ps_pool", bufs=1))
        ctx.enter_context(tc.manual_schedule())

        xbytes, wraw, xwide, xgrp, wgrp, txs, wps = {}, {}, {}, {}, {}, {}, {}
        xcod, xscl, wcod, wscl = {}, {}, {}, {}
        acc, tt, r1s, i1s, tos, ots = {}, {}, {}, {}, {}, {}

        def bank(tag, cols, dt=F32):
            return ps_pool.tile([P, cols], dt, name=tag, tag=tag)

        sct = const.tile([P, 1, 2, 2], F32, name="sct", tag="sct")
        nc.scalar.dma_start(
            out=sct[:].rearrange("p o u e -> p (o u e)"),
            in_=x_crop_scale.rearrange("a b c d (p t) -> p (a b c d t)", t=4),
        )
        brb = const.tile([P, 1], BF16, name="brb", tag="brb")
        bib = const.tile([P, 1], BF16, name="bib", tag="bib")

        def load_bias():
            nc.scalar.dma_start(out=brb[:], in_=b_r.rearrange("(f o) -> f o", o=1))
            nc.scalar.dma_start(out=bib[:], in_=b_i.rearrange("(f o) -> f o", o=1))

        if not LATE_BIAS:
            load_bias()
        if WARM_PE:
            wz = const.tile([P, C], BF16, name="wz", tag="wz")
            nc.vector.memset(wz[:], 0.0)
            dummy = bank("to", C)
            for k in range(WARM_PE):
                nc.tensor.matmul(dummy[:], lhsT=wz[:, 0:P], rhs=wz[:], start=True, stop=True)
        ident = const.tile([P, P], F32, name="ident", tag="ident")
        make_identity(nc, ident[:])
        identb = const.tile([P, P], BF16, name="identb", tag="identb")
        nc.vector.tensor_copy(out=identb[:], in_=ident[:])
        warm = const.tile([P, 1], F32, name="warm", tag="warm")
        warm2 = const.tile([P, 1], F32, name="warm2", tag="warm2")
        nc.gpsimd.memset(warm[:], 0.0)
        nc.scalar.activation(out=warm2[:], in_=warm[:], func=ACT.Relu)
        brc = const.tile([P, 1], F32, name="brc", tag="brc")
        bic = const.tile([P, 1], F32, name="bic", tag="bic")

        def load_x(g, w0, w1):
            if g not in xbytes:
                xbytes[g] = xb_pool.tile([P, 2 * GW], U8, name="xbytes", tag="xbytes")
            nc.sync.dma_start(
                out=xbytes[g][:].rearrange("p (c n) -> p c n", c=2)[:, :, w0 * C:w1 * C],
                in_=x_crop_bytes[:, :, g, w0:w1, :].rearrange("b c w k -> b c (w k)"),
            )

        def load_w(g, m, w0=0, w1=WC):
            if g not in wraw:
                wraw[g] = wr_pool.tile([P, 2, WC, 4 * F], BF16, name="wraw", tag="wraw")
            src = (W_r, W_i)[m]
            nc.sync.dma_start(out=wraw[g][:, m, w0:w1], in_=src[g, w0:w1].rearrange("w (p j) f -> p w (j f)", j=4))

        def cast(g, lo, hi, on_vector=False):
            if g not in xwide:
                xwide[g] = xw_pool.tile([P, 2 * GW], BF16, name="xw", tag="xw", align_bytes=64)
            dst = xwide[g][:, lo:hi]
            src = xbytes[g][:, lo:hi].bitcast(FP8)
            if on_vector:
                nc.vector.tensor_copy(out=dst, in_=src)
            else:
                nc.scalar.copy(out=dst, in_=src)

        def cast_px(g, w0, w1, on_vector=False):
            cast(g, w0 * C, w1 * C, on_vector)
            cast(g, GW + w0 * C, GW + w1 * C, on_vector)

        def txp(g, ws=(0, 1, 2, 3)):
            words = xwide[g][:].bitcast(F32)
            for w in ws:
                tx = bank("tx%d" % w, 4 * P)
                for u in range(2):
                    for c in range(2):
                        off = (c * WC + w) * (C // 2)
                        nc.tensor.transpose(
                            tx[:, (2 * u + c) * P:(2 * u + c + 1) * P],
                            words[:, off + u:off + C // 2:2],
                            ident[:],
                        )
                txs[g, w] = tx

        def new_xg(g):
            if g not in xgrp:
                xgrp[g] = xg_pool.tile([P, 2 * GW], BF16, name="xg", tag="xg", align_bytes=64)

        def em(g, ws=(0, 1, 2, 3)):
            new_xg(g)
            xg = xgrp[g]
            for w in ws:
                if w in P_EM.get(g, ()):
                    continue
                nc.vector.tensor_tensor(
                    out=xg[:, w * 2 * C:(w + 1) * 2 * C].rearrange("p (n u e) -> p n u e", u=2, e=2),
                    in0=sct[:].to_broadcast([P, 2 * P, 2, 2]),
                    in1=txs[g, w][:].bitcast(BF16).rearrange("p (u n e) -> p n u e", u=2, e=2),
                    op=ALU.mult,
                )

        xpl, xpp = {}, {}

        def em_p_planes(g):
            for w in P_EM.get(g, ()):
                xpl[g, w] = pl_pool.tile([P, 4, 2 * P], BF16, name="xpl", tag="xpl")
                for t in range(4):
                    nc.scalar.activation(
                        out=xpl[g, w][:, t, :],
                        in_=txs[g, w][:].bitcast(BF16).rearrange("p (u n e) -> p u n e", u=2, e=2)[:, t // 2, :, t % 2],
                        func=ACT.Copy,
                        scale=sct[:].rearrange("p o u e -> p (o u e)")[:, t:t + 1],
                    )

        def em_p_mm(g):
            for w in P_EM.get(g, ()):
                xpp[g, w] = bank("rr", 2 * C, BF16)
                for h in range(2):
                    nc.tensor.matmul(
                        xpp[g, w][:, h * C:(h + 1) * C], lhsT=identb[:],
                        rhs=xpl[g, w][:, :, h * P:(h + 1) * P].rearrange("p t n -> p n t"),
                        start=True, stop=True,
                    )

        def em_p_cp(g):
            for w in P_EM.get(g, ()):
                nc.scalar.copy(out=xgrp[g][:, w * 2 * C:(w + 1) * 2 * C], in_=xpp[g, w][:])

        def il_views(g, u0, u1):
            dst = wgrp[g][:, u0 * C:u1 * C].rearrange("p (w f j) -> p w f j", w=u1 - u0, j=4)
            src = wraw[g][:].rearrange("p m w n -> p (m w) n")[:, u0:u1, :].rearrange("p w (j f) -> p w f j", j=4)
            return dst, src

        def wil_g(g, cuts=None):
            if g not in wgrp:
                wgrp[g] = wg_pool.tile([P, 2 * GW], BF16, name="wg", tag="wg", align_bytes=64)
            cuts = cuts or (0, G_UNITS[g])
            for a, b_ in zip(cuts[:-1], cuts[1:]):
                dst, src = il_views(g, a, b_)
                nc.gpsimd.tensor_scalar(out=dst, in0=src, scalar1=1.0, scalar2=0.0, op0=ALU.mult, op1=ALU.add)

        def wil_s(g):
            u0 = G_UNITS[g] + PE_UNITS[g]
            if u0 < 8:
                dst, src = il_views(g, u0, 8)
                nc.scalar.copy(out=dst, in_=src)

        def wpe_mm(g, tag="ii"):
            n = PE_UNITS[g]
            if n:
                wp = bank(tag, n * C, BF16)
                for i in range(n):
                    u = G_UNITS[g] + i
                    nc.tensor.matmul(
                        wp[:, i * C:(i + 1) * C], lhsT=identb[:],
                        rhs=wraw[g][:].rearrange("p m w n -> p (m w) n")[:, u, :].rearrange("p (j f) -> p f j", j=4),
                        start=True, stop=True,
                    )
                wps[g] = wp

        def wpe_cp(g):
            if g in wps:
                u, n = G_UNITS[g], PE_UNITS[g]
                nc.scalar.copy(out=wgrp[g][:, u * C:(u + n) * C], in_=wps[g][:])

        def quant_x(g, w0, w1):
            if g not in xcod:
                xcod[g] = cd_pool.tile([P, 2 * WC * P], U32, name="xc", tag="xc", align_bytes=64)
                xscl[g] = cd_pool.tile([P, 2 * WC * P], U8, name="xs", tag="xs", align_bytes=64)
            lo, hi = 2 * w0 * P, 2 * w1 * P
            nc.vector.quantize_mx(out=xcod[g][:, lo:hi].bitcast(FP8X4), scales=xscl[g][:, lo:hi], in_=xgrp[g][:, 4 * lo:4 * hi])

        def quant_w(g):
            cod = cd_pool.tile([P, 2 * WC * F], U32, name="wc", tag="wc", align_bytes=64)
            scl = cd_pool.tile([P, 2 * WC * F], U8, name="ws", tag="ws", align_bytes=64)
            nc.vector.quantize_mx(out=cod[:].bitcast(FP8X4), scales=scl[:], in_=wgrp[g][:])
            wcod[g], wscl[g] = cod, scl

        def mm(g, ws=(0, 1, 2, 3), tags=("rr", "ii", "pi")):
            n = len(ws)
            rr = bank(tags[0], n * P)
            ii = bank(tags[1], n * P)
            pi = bank(tags[2], n * P)
            acc[g, ws] = (rr, ii, pi)

            def mx(dst, w, m, c, start, stop):
                ws_ = slice((m * WC + w) * F, (m * WC + w + 1) * F)
                xs_ = slice((2 * w + c) * P, (2 * w + c + 1) * P)
                nc.tensor.matmul_mx(
                    out=dst[:, (w - ws[0]) * P:(w - ws[0] + 1) * P],
                    lhsT=wcod[g][:, ws_].bitcast(FP8X4),
                    lhsT_scale=wscl[g][:, ws_],
                    rhs=xcod[g][:, xs_].bitcast(FP8X4),
                    rhs_scale=xscl[g][:, xs_],
                    start=start,
                    stop=stop,
                )

            for w in ws:
                mx(ii, w, 1, 1, True, True)
            for w in ws:
                mx(rr, w, 0, 0, True, True)
            for w in ws:
                mx(pi, w, 0, 1, True, False)
                mx(pi, w, 1, 0, False, True)

        ALLW = (0, 1, 2, 3)

        def e1_t(g, ws=ALLW):
            t = ep_pool.tile([P, len(ws) * P], F32, name="t", tag="t")
            nc.scalar.activation(out=t[:], in_=acc[g, ws][1][:], func=ACT.Identity, bias=brc[:], scale=-1.0)
            tt[g, ws] = t

        def e1_r(g, ws=ALLW, on_vector=False):
            r = ep_pool.tile([P, len(ws) * P], F32, name="r1", tag="r1")
            if on_vector:
                nc.vector.tensor_copy(out=r[:], in_=acc[g, ws][0][:])
            else:
                nc.scalar.copy(out=r[:], in_=acc[g, ws][0][:])
            r1s[g, ws] = r

        def e1_i(g, ws=ALLW, on_vector=False):
            i1 = ep_pool.tile([P, len(ws) * P], F32, name="i1", tag="i1")
            if on_vector:
                nc.vector.tensor_scalar(out=i1[:], in0=acc[g, ws][2][:], scalar1=bic[:], scalar2=0.0, op0=ALU.add, op1=ALU.max)
            else:
                nc.scalar.activation(out=i1[:], in_=acc[g, ws][2][:], func=ACT.Relu, bias=bic[:], scale=1.0)
            i1s[g, ws] = i1

        def back_r(to, col, g, ws):
            for k in range(len(ws)):
                dst = to[:, (col + k) * F:(col + k + 1) * F]
                nc.tensor.matmul(dst, lhsT=r1s[g, ws][:, k * P:(k + 1) * P], rhs=ident[:], start=True, stop=False, is_transpose=True)
                nc.tensor.matmul(dst, lhsT=tt[g, ws][:, k * P:(k + 1) * P], rhs=ident[:], start=False, stop=True, is_transpose=True)

        def back_i(to, col, g, ws):
            for k in range(len(ws)):
                nc.tensor.transpose(to[:, (col + k) * F:(col + k + 1) * F], i1s[g, ws][:, k * P:(k + 1) * P], ident[:])

        def tout_r(g, tag="to"):
            tos[g] = bank(tag, WC * F)
            back_r(tos[g], 0, g, ALLW)

        def tout_i(g, tag="to"):
            tos[g] = bank(tag, WC * F)
            back_i(tos[g], 0, g, ALLW)

        def e2i(g):
            if g not in ots:
                ots[g] = ot_pool.tile([P, 2 * WC * F], F32, name="ot", tag="ot")
            nc.scalar.copy(out=ots[g][:, WC * F:], in_=tos[g][:])

        def e2r(g):
            if g not in ots:
                ots[g] = ot_pool.tile([P, 2 * WC * F], F32, name="ot", tag="ot")
            nc.scalar.activation(out=ots[g][:, 0:WC * F], in_=tos[g][:], func=ACT.Relu)

        def store(g):
            nc.sync.dma_start(
                out=out[:, :, g, :, :].rearrange("b c w f -> b c (w f)"),
                in_=ots[g][:].rearrange("p (c n) -> p c n", c=2),
            )

        pto = {}

        def tout_piece(g, ws, tag):
            n = len(ws)
            to = bank(tag, 2 * n * F)
            back_r(to, 0, g, ws)
            back_i(to, n, g, ws)
            pto[ws] = to

        def e2_piece(g, ws, on_vector=False):
            n = len(ws)
            o = ot_pool.tile([P, 2 * n * F], F32, name="ot", tag="ot")
            if on_vector:
                nc.vector.tensor_scalar_max(out=o[:], in0=pto[ws][:], scalar1=0.0)
            else:
                nc.scalar.activation(out=o[:], in_=pto[ws][:], func=ACT.Relu)
            nc.sync.dma_start(
                out=out[:, :, g, ws[0]:ws[0] + n, :].rearrange("b c w f -> b c (w f)"),
                in_=o[:].rearrange("p (c n) -> p c n", c=2),
            )

        def last_pixel(g, w, tags=("rr", "ii")):
            za = bank(tags[0], 2 * F)
            zb = bank(tags[1], F)

            def mx(dst, m, c, start, stop):
                ws_ = slice((m * WC + w) * F, (m * WC + w + 1) * F)
                xs_ = slice((2 * w + c) * P, (2 * w + c + 1) * P)
                nc.tensor.matmul_mx(
                    out=dst,
                    lhsT=xcod[g][:, xs_].bitcast(FP8X4),
                    lhsT_scale=xscl[g][:, xs_],
                    rhs=wcod[g][:, ws_].bitcast(FP8X4),
                    rhs_scale=wscl[g][:, ws_],
                    start=start,
                    stop=stop,
                )

            mx(zb[:], 1, 1, True, True)
            mx(za[:, 0:F], 0, 0, True, True)
            mx(za[:, F:2 * F], 0, 1, True, False)
            mx(za[:, F:2 * F], 1, 0, False, True)
            t = ep_pool.tile([P, F], F32, name="t", tag="t")
            z = ep_pool.tile([P, 2 * F], F32, name="r1", tag="r1")
            o = ot_pool.tile([P, 2 * F], F32, name="ot", tag="ot")
            nc.vector.tensor_tensor(out=t[:], in0=bb[:, 0:F], in1=zb[:], op=ALU.subtract)
            nc.vector.tensor_tensor(out=z[:, F:2 * F], in0=za[:, F:2 * F], in1=bb[:, F:2 * F], op=ALU.add)
            nc.vector.tensor_tensor(out=z[:, 0:F], in0=za[:, 0:F], in1=t[:], op=ALU.add)
            if LASTX == 2:
                nc.scalar.activation(out=o[:, F:2 * F], in_=z[:, F:2 * F], func=ACT.Relu)
                nc.vector.tensor_scalar_max(out=o[:, 0:F], in0=z[:, 0:F], scalar1=0.0)
            else:
                nc.vector.tensor_scalar_max(out=o[:], in0=z[:], scalar1=0.0)
            return o

        def last_store(g, w, o):
            nc.sync.dma_start(
                out=out[:, :, g, w:w + 1, :].rearrange("b c w f -> b c (w f)"),
                in_=o[:].rearrange("p (c n) -> p c n", c=2),
            )

        def quants(g):
            if QW_FIRST:
                quant_w(g)
                quant_x(g, 0, 4)
            else:
                quant_x(g, 0, 2)
                quant_w(g)
                quant_x(g, 2, 4)

        load_x(0, 0, 1)
        load_x(0, 1, 2)
        load_w(0, 0, 0, 2)
        load_x(0, 2, WC)
        load_w(0, 0, 2, 4)
        load_w(0, 1)
        load_x(1, 0, WC)
        for g in range(2, HC):
            load_w(g - 1, 0)
            load_w(g - 1, 1)
            load_x(g, 0, WC)
        load_w(HC - 1, 0)
        load_w(HC - 1, 1)
        if LASTX:
            bb = const.tile([P, 2 * F], BF16, name="bb", tag="bb")
            nc.sync.dma_start(out=bb[:, 0:F], in_=b_r.partition_broadcast(P))
            nc.sync.dma_start(out=bb[:, F:2 * F], in_=b_i.partition_broadcast(P))

        if NEW_HEAD >= 1:
            cast(0, 0, C, on_vector=True)
            cast(0, GW, GW + C)
        else:
            cast_px(0, 0, 1, on_vector=True)
        cast_px(0, 1, 2)
        if NEW_HEAD >= 2:
            cast_px(0, 2, 3)
            cast_px(0, 3, 4)
        else:
            cast_px(0, 2, 4)
        if LATE_BIAS:
            load_bias()
        wil_g(0, (0, 2, WC, G_UNITS[0]))
        txp(0)
        wil_s(0)
        cast_px(1, 0, 2)
        cast_px(1, 2, 4)
        nc.scalar.copy(out=brc[:], in_=brb[:])
        nc.scalar.copy(out=bic[:], in_=bib[:])
        em(0)
        txp(1)
        last = HC - 1
        for j in range(last):
            more = j + 2 < HC
            quants(j)
            wil_g(j + 1)
            if j in WS_FIRST:
                wil_s(j + 1)
            if P_AT == 0:
                em_p_planes(j + 1)
            if more:
                cast(j + 2, 0, GW)
            if P_AT == 1:
                em_p_planes(j + 1)
            if j not in WS_FIRST:
                wil_s(j + 1)
            if j >= 1:
                e2i(j - 1)
            mm(j)
            if j >= 1:
                tout_r(j - 1)
            e1_t(j)
            e1_r(j)
            wpe_mm(j + 1)
            em_p_mm(j + 1)
            if more:
                cast(j + 2, GW, GW + GW // 2)
            wpe_cp(j + 1)
            new_xg(j + 1)
            em_p_cp(j + 1)
            if more:
                cast(j + 2, GW + GW // 2, 2 * GW)
            e1_i(j)
            if j >= 1:
                e2r(j - 1)
                store(j - 1)
            if j < last - 1:
                em(j + 1)
            else:
                if TQ == 2:
                    em(last, (0, 1))
                    quant_x(last, 0, 2)
                    quant_w(last)
                    em(last, (2,))
                else:
                    em(last, (0, 1, 2))
                if TQ == 2:
                    pass
                elif TQ:
                    quant_x(last, 0, 2)
                    quant_w(last)
                else:
                    quant_w(last)
                    quant_x(last, 0, 2)
                quant_x(last, 2, 3)
                em(last, (3,))
                quant_x(last, 3, 4)
            if more:
                txp(j + 2)
            if not (NEW_TAIL and j == last - 1):
                tout_i(j)

        pa, pb, pc = (0, 1), (2,), (3,)
        if NEW_TAIL:
            tout_r(last - 1, "tx0")
            e2r(last - 1)
            tout_i(last - 1, "tx1")
            e2i(last - 1)
            store(last - 1)
            mm(last, pa)
            e1_t(last, pa)
            e1_r(last, pa)
            e1_i(last, pa)
            if LASTX == 3:
                o2 = last_pixel(last, 2, ("tx2", "to"))
                tout_piece(last, pa, "tx1")
                o3 = last_pixel(last, 3)
                last_store(last, 2, o2)
                e2_piece(last, pa)
                last_store(last, 3, o3)
                return
            mm(last, pb, ("tx2", "to", "tx0"))
            tout_piece(last, pa, "tx1")
            e1_t(last, pb)
            e1_r(last, pb, on_vector=TV >= 2)
            e1_i(last, pb)
            if LASTX:
                o3 = last_pixel(last, 3)
                e2_piece(last, pa)
                tout_piece(last, pb, "tx3")
                e2_piece(last, pb)
                last_store(last, 3, o3)
                return
            mm(last, pc)
            e2_piece(last, pa, on_vector=TV >= 1)
            tout_piece(last, pb, "tx3")
            e1_t(last, pc)
            e1_r(last, pc, on_vector=RPC_V)
            e1_i(last, pc, on_vector=TV >= 3)
            e2_piece(last, pb, on_vector=TV >= 1)
            tout_piece(last, pc, "tx2")
            e2_piece(last, pc)
            return
        e2i(last - 1)
        mm(last, pa)
        tout_r(last - 1)
        e1_t(last, pa)
        e1_r(last, pa)
        e1_i(last, pa)
        mm(last, pb, ("tx1", "tx0", "tx2"))
        e2r(last - 1)
        store(last - 1)
        tout_piece(last, pa, "tx3")
        e1_t(last, pb)
        e1_r(last, pb)
        e1_i(last, pb)
        mm(last, pc)
        e2_piece(last, pa)
        tout_piece(last, pb, "to")
        e1_t(last, pc)
        e1_r(last, pc, on_vector=True)
        e1_i(last, pc)
        e2_piece(last, pb)
        tout_piece(last, pc, "tx0")
        e2_piece(last, pc)
